import numpy as np
import ml_dtypes


def mxq(x, axis, fmt="e4m3"):
    dtype, down = {"e4m3": (ml_dtypes.float8_e4m3fn, 7), "e5m2": (ml_dtypes.float8_e5m2, 14)}[fmt]
    v = np.moveaxis(np.asarray(x, np.float32).astype(ml_dtypes.bfloat16).astype(np.float64), axis, -1)
    blocks = v.reshape(v.shape[:-1] + (-1, 32))
    amax = np.abs(blocks).max(-1, keepdims=True)
    byte = np.maximum(np.where(amax > 0, np.frexp(amax)[1] - 1 + 127, 0) - down, 1)
    scale = np.exp2(byte - 127.0)
    codes = (blocks / scale).astype(np.float32).astype(dtype).astype(np.float64)
    return np.moveaxis((codes * scale).reshape(v.shape), -1, axis)


WIDE = False


def mx_kscale(k):
    if not WIDE:
        return np.ones(k)
    levels = np.array([10, -10, 5, -5, 0])
    a = np.random.permutation(np.resize(levels, k // 512 * 4)).reshape(k // 512, 4)
    idx = np.arange(k)
    return np.exp2(a[idx // 512, idx % 128 // 32])


BF16 = ml_dtypes.bfloat16


def bf(x):
    return np.asarray(x, np.float32).astype(BF16)


def f64(x):
    return np.asarray(x).astype(np.float64)


E2M1 = np.array([0.0, 0.5, 1.0, 1.5, 2.0, 3.0, 4.0, 6.0, -0.0, -0.5, -1.0, -1.5, -2.0, -3.0, -4.0, -6.0])


def pack_weight(w, fmt):
    k, n = w.shape
    w = f64(bf(w)).reshape(k // 32, 32, n)
    amax = np.abs(w).max(1)
    if fmt == "e4m3":
        byte = np.frexp(amax)[1] - 1 + 127 - 7
    else:
        mant, ex = np.frexp(amax / 6.0)
        byte = np.where(mant > 0.5, ex, ex - 1) + 127
    byte = np.clip(np.where(amax > 0, byte, 1), 1, 254)
    scaled = (w * np.exp2(127.0 - byte)[:, None, :]).reshape(k, n).astype(np.float32)
    by_word = np.ascontiguousarray(scaled.reshape(k // 512, 128, 4, n).transpose(0, 1, 3, 2))
    if fmt == "e4m3":
        words = by_word.astype(ml_dtypes.float8_e4m3fn).view(np.uint8)
    else:
        c = by_word.astype(ml_dtypes.float4_e2m1fn).view(np.uint8) & 0xF
        words = c[..., 0::2] | (c[..., 1::2] << 4)
    return np.ascontiguousarray(words), np.ascontiguousarray(byte.astype(np.uint8).reshape(k // 512, 16, n))


def unpack_weight(words, scales, fmt):
    g, p, n, _ = words.shape
    if fmt == "e4m3":
        vals = np.ascontiguousarray(words).view(ml_dtypes.float8_e4m3fn).astype(np.float64)
    else:
        nib = np.empty((g, p, n, 4), np.uint8)
        nib[..., 0::2] = words & 0xF
        nib[..., 1::2] = words >> 4
        vals = E2M1[nib]
    vals = vals * np.repeat(np.exp2(scales.astype(np.float64) - 127.0), 8, axis=1)[..., None]
    return vals.transpose(0, 1, 3, 2).reshape(g * 512, n)

def pack4(w):
    words, scales = pack_weight(w, "e2m1")
    return words.reshape(words.shape[0], 128, -1), scales


def unpack4(words, scales):
    return unpack_weight(words.reshape(words.shape[0], 128, -1, 2), scales, "e2m1")


B, IN, H, G, GA, GB = 4096, 1024, 512, 6, 4, 2
EPS = 1e-5


def layer_norm(v, g, b):
    mu = v.mean(-1, keepdims=True)
    var = np.square(v - mu).mean(-1, keepdims=True)
    return (v - mu) / np.sqrt(var + EPS) * g + b


def sigmoid(v):
    return 1.0 / (1.0 + np.exp(-v))


def setup_inputs():
    s = mx_kscale(IN)
    x = bf(np.random.standard_normal((B, IN)) * s)
    h = bf(np.random.standard_normal((B, H)))
    c = bf(np.tanh(1.4 * np.random.standard_normal((B, H))))
    W_u_words, W_u_scales = pack4((np.random.standard_normal((H, H)) / np.sqrt(H)).T)
    U_u_words, U_u_scales = pack4((np.random.standard_normal((H, IN)) / np.sqrt(IN) / s).T)
    ln_gamma = bf(1.0 + 0.1 * np.random.standard_normal((GB, H)))
    ln_beta = bf(0.2 * np.random.standard_normal((GB, H)))
    return {"x": x,
            "h": h,
            "c": c,
            "W_u_words": W_u_words,
            "W_u_scales": W_u_scales,
            "U_u_words": U_u_words,
            "U_u_scales": U_u_scales,
            "ln_gamma": ln_gamma,
            "ln_beta": ln_beta}


def reference(x, h, c, W_u_words, W_u_scales, U_u_words, U_u_scales, ln_gamma, ln_beta):
    g_uh, g_ux = f64(ln_gamma)
    b_uh, b_ux = f64(ln_beta)
    hf = f64(h)
    u = sigmoid(layer_norm(mxq(hf, 1, "e4m3") @ unpack4(W_u_words, W_u_scales), g_uh, b_uh)
                + layer_norm(mxq(f64(x), 1, "e4m3") @ unpack4(U_u_words, U_u_scales), g_ux, b_ux))
    return (1.0 - u) * hf + u * f64(c)

@@ -1,0 +1,253 @@
+from contextlib import ExitStack
+
+import concourse.masks as masks
+import concourse.mybir as mybir
+
+F32 = mybir.dt.float32
+BF16 = mybir.dt.bfloat16
+I32 = mybir.dt.int32
+U32 = mybir.dt.uint32
+U8 = mybir.dt.uint8
+FP8X4 = mybir.dt.float8_e4m3fn_x4
+FP4X4 = mybir.dt.float4_e2m1fn_x4
+ACT = mybir.ActivationFunctionType
+ALU = mybir.AluOpType
+
+P = 128
+ROWS, IN, H = 4096, 1024, 512
+EPS = 1e-5
+K_PASS = 4 * P
+X_PASSES = IN // K_PASS
+WORDS = K_PASS // 2
+GROUP_TILES = 4
+N_GROUPS = ROWS // (P * GROUP_TILES)
+N_TILES = ROWS // P
+
+FLOPS = 2 * ROWS * H * (H + IN)
+
+
+def tile_layernormgrucell_pb_t_kernel(
+    tc, x, h, c, W_u_words, W_u_scales, U_u_words, U_u_scales, ln_gamma, ln_beta, out
+):
+    nc = tc.nc
+
+    x_groups = x.rearrange("(g p t) k -> g p t k", p=P, t=GROUP_TILES)
+    h_groups = h.rearrange("(g p t) k -> g p t k", p=P, t=GROUP_TILES)
+    c_groups = c.rearrange("(g p t) k -> g p t k", p=P, t=GROUP_TILES)
+    out_groups = out.rearrange("(g p t) n -> g p t n", p=P, t=GROUP_TILES)
+
+    with ExitStack() as ctx:
+        const = ctx.enter_context(tc.tile_pool(name="const", bufs=1))
+        x_pool = ctx.enter_context(tc.tile_pool(name="x_pool", bufs=3))
+        hc_pool = ctx.enter_context(tc.tile_pool(name="hc_pool", bufs=4))
+        quant = ctx.enter_context(tc.tile_pool(name="quant", bufs=2))
+        unread = ctx.enter_context(tc.tile_pool(name="unread", bufs=4))
+        small = ctx.enter_context(tc.tile_pool(name="small", bufs=3))
+        work = ctx.enter_context(tc.tile_pool(name="work", bufs=4))
+        psum = ctx.enter_context(tc.psum_pool(name="psum", bufs=2))
+        ctx.enter_context(tc.manual_schedule())
+
+        x_sb, h_sb, c_sb = {}, {}, {}
+
+        def load(g):
+            h_sb[g] = hc_pool.tile([P, GROUP_TILES, H], BF16, name="h_rows")
+            nc.sync.dma_start(out=h_sb[g][:], in_=h_groups[g])
+            x_sb[g] = x_pool.tile([P, GROUP_TILES, IN], BF16, name="x_rows")
+            nc.sync.dma_start(out=x_sb[g][:], in_=x_groups[g])
+            c_sb[g] = hc_pool.tile([P, GROUP_TILES, H], BF16, name="c_rows")
+            nc.sync.dma_start(out=c_sb[g][:], in_=c_groups[g])
+
+        w_scales = const.tile([P, 1 + X_PASSES, H], U8, align_bytes=64)
+        nc.vector.memset(w_scales[:].rearrange("p w n -> p (w n)").bitcast(I32), 0)
+        neg_half = const.tile([P, 2], F32)
+        nc.vector.memset(neg_half[:], -0.5)
+        ident = const.tile([P, P], F32)
+        masks.make_identity(nc, ident[:])
+
+        load(0)
+        w_words = const.tile([P, 1 + X_PASSES, 2 * H], U8, align_bytes=64)
+        for q in range(4):
+            nc.sync.dma_start(
+                out=w_scales[32 * q : 32 * q + 4, 0, :].bitcast(I32),
+                in_=W_u_scales[0, 4 * q : 4 * q + 4, :].bitcast(I32),
+            )
+        nc.sync.dma_start(out=w_words[:, 0, :].bitcast(I32), in_=W_u_words[0].bitcast(I32))
+        for q in range(4):
+            nc.sync.dma_start(
+                out=w_scales[32 * q : 32 * q + 4, 1:, :].bitcast(I32),
+                in_=U_u_scales[:, 4 * q : 4 * q + 4, :].rearrange("g r n -> r g n").bitcast(I32),
+            )
+        for g in range(X_PASSES):
+            nc.sync.dma_start(out=w_words[:, 1 + g, :].bitcast(I32), in_=U_u_words[g].bitcast(I32))
+        gamma = const.tile([P, 2, H], BF16)
+        nc.sync.dma_start(
+            out=gamma[:].rearrange("p i n -> p (i n)"),
+            in_=ln_gamma.rearrange("i n -> (i n)").partition_broadcast(P),
+        )
+        beta = const.tile([P, 2, H], BF16)
+        nc.sync.dma_start(
+            out=beta[:].rearrange("p i n -> p (i n)"),
+            in_=ln_beta.rearrange("i n -> (i n)").partition_broadcast(P),
+        )
+        beta_sum = const.tile([P, H], F32)
+        nc.gpsimd.tensor_tensor(out=beta_sum[:], in0=beta[:, 0, :], in1=beta[:, 1, :], op=ALU.add)
+        load(1)
+
+        xT, hT = {}, {}
+        x_grouped, h_grouped = {}, {}
+        x_codes, x_scales, h_codes, h_scales = {}, {}, {}, {}
+        acc_h, acc_x = {}, {}
+        neg_mean, sq_sum, rstd = {}, {}, {}
+        hid, gate, diff = {}, {}, {}
+
+        def transposes(i):
+            g, t = divmod(i, GROUP_TILES)
+            x_words = x_sb[g][:, t, :].bitcast(F32)
+            h_words = h_sb[g][:, t, :].bitcast(F32)
+            xT[i] = psum.tile([P, X_PASSES, 2, P], F32, name="xT")
+            hT[i] = psum.tile([P, 2, P], F32, name="hT")
+            for u in range(2):
+                nc.tensor.transpose(hT[i][:, u, :], h_words[:, u:WORDS:2], ident[:])
+            for s in range(X_PASSES):
+                for u in range(2):
+                    nc.tensor.transpose(
+                        xT[i][:, s, u, :], x_words[:, s * WORDS + u : (s + 1) * WORDS : 2], ident[:]
+                    )
+
+        def copy_h(i):
+            h_grouped[i] = quant.tile([P, 4 * P], BF16, name="h_grouped", align_bytes=64)
+            nc.scalar.copy(
+                out=h_grouped[i][:].bitcast(F32).rearrange("p (r u) -> p r u", u=2),
+                in_=hT[i][:].rearrange("p u r -> p r u"),
+            )
+
+        def copy_x(i):
+            x_grouped[i] = quant.tile([P, X_PASSES * 4 * P], BF16, name="x_grouped", align_bytes=64)
+            nc.scalar.copy(
+                out=x_grouped[i][:].bitcast(F32).rearrange("p (s r u) -> p s r u", s=X_PASSES, u=2),
+                in_=xT[i][:].rearrange("p s u r -> p s r u"),
+            )
+
+        def quantise(i):
+            h_codes[i] = quant.tile([P, P], U32, name="h_codes", align_bytes=64)
+            h_scales[i] = quant.tile([P, P], U8, name="h_scales", align_bytes=64)
+            nc.vector.quantize_mx(out=h_codes[i][:].bitcast(FP8X4), scales=h_scales[i][:], in_=h_grouped[i][:])
+            x_codes[i] = quant.tile([P, X_PASSES * P], U32, name="x_codes", align_bytes=64)
+            x_scales[i] = quant.tile([P, X_PASSES * P], U8, name="x_scales", align_bytes=64)
+            nc.vector.quantize_mx(out=x_codes[i][:].bitcast(FP8X4), scales=x_scales[i][:], in_=x_grouped[i][:])
+
+        def matmuls(i):
+            acc_h[i] = psum.tile([P, H], F32, name="acc_h")
+            nc.tensor.matmul_mx(
+                out=acc_h[i][:],
+                lhsT=h_codes[i][:].bitcast(FP8X4),
+                lhsT_scale=h_scales[i][:],
+                rhs=w_words[:, 0, :].bitcast(FP4X4),
+                rhs_scale=w_scales[:, 0, :],
+                start=True,
+                stop=True,
+            )
+            acc_x[i] = psum.tile([P, H], F32, name="acc_x")
+            for s in range(X_PASSES):
+                cols = slice(s * P, (s + 1) * P)
+                nc.tensor.matmul_mx(
+                    out=acc_x[i][:],
+                    lhsT=x_codes[i][:, cols].bitcast(FP8X4),
+                    lhsT_scale=x_scales[i][:, cols],
+                    rhs=w_words[:, 1 + s, :].bitcast(FP4X4),
+                    rhs_scale=w_scales[:, 1 + s, :],
+                    start=(s == 0),
+                    stop=(s == X_PASSES - 1),
+                )
+
+        def means(i):
+            sums = small.tile([P, 2], F32, name="sums")
+            for col, acc in enumerate((acc_h[i], acc_x[i])):
+                scrap = unread.tile([P, H], F32, name="scrap")
+                nc.scalar.activation(out=scrap[:], in_=acc[:], func=ACT.Identity, accum_out=sums[:, col : col + 1])
+            neg_mean[i] = small.tile([P, 2], F32, name="neg_mean")
+            nc.scalar.mul(out=neg_mean[i][:], in_=sums[:], mul=-1.0 / H)
+
+        def squares(i):
+            sq_sum[i] = small.tile([P, 2], F32, name="sq_sum")
+            for col, acc in enumerate((acc_h[i], acc_x[i])):
+                scrap = unread.tile([P, H], F32, name="scrap")
+                nc.scalar.activation(
+                    out=scrap[:],
+                    in_=acc[:],
+                    func=ACT.Square,
+                    bias=neg_mean[i][:, col : col + 1],
+                    scale=1.0,
+                    accum_out=sq_sum[i][:, col : col + 1],
+                )
+
+        def centre(i):
+            hid[i] = work.tile([P, H], F32, name="hid")
+            gate[i] = work.tile([P, H], F32, name="gate")
+            for col, (acc, dst) in enumerate(((acc_h[i], hid[i]), (acc_x[i], gate[i]))):
+                nc.vector.scalar_tensor_tensor(
+                    out=dst[:],
+                    in0=acc[:],
+                    scalar=neg_mean[i][:, col : col + 1],
+                    in1=gamma[:, col, :],
+                    op0=ALU.add,
+                    op1=ALU.mult,
+                )
+
+        def inverse_deviation(i):
+            var_eps = small.tile([P, 2], F32, name="var_eps")
+            nc.gpsimd.tensor_scalar(
+                out=var_eps[:], in0=sq_sum[i][:], scalar1=1.0 / H, scalar2=EPS, op0=ALU.mult, op1=ALU.add
+            )
+            rstd[i] = small.tile([P, 2], F32, name="rstd")
+            nc.gpsimd.tensor_tensor(out=rstd[i][:], in0=var_eps[:], in1=neg_half[:], op=ALU.pow)
+
+        def difference(i):
+            g, t = divmod(i, GROUP_TILES)
+            diff[i] = work.tile([P, H], F32, name="diff")
+            nc.gpsimd.tensor_tensor(out=diff[i][:], in0=c_sb[g][:, t, :], in1=h_sb[g][:, t, :], op=ALU.subtract)
+
+        def add_hidden_norm(i):
+            nc.vector.scalar_tensor_tensor(
+                out=hid[i][:], in0=hid[i][:], scalar=rstd[i][:, 0:1], in1=beta_sum[:], op0=ALU.mult, op1=ALU.add
+            )
+
+        def add_input_norm(i):
+            nc.vector.scalar_tensor_tensor(
+                out=gate[i][:], in0=gate[i][:], scalar=rstd[i][:, 1:2], in1=hid[i][:], op0=ALU.mult, op1=ALU.add
+            )
+
+        def sigmoid(i):
+            nc.scalar.activation(out=gate[i][:], in_=gate[i][:], func=ACT.Sigmoid)
+
+        def weigh_difference(i):
+            nc.vector.tensor_tensor(out=gate[i][:], in0=gate[i][:], in1=diff[i][:], op=ALU.mult)
+
+        def add_state_and_store(i):
+            g, t = divmod(i, GROUP_TILES)
+            nc.vector.tensor_tensor(out=gate[i][:], in0=gate[i][:], in1=h_sb[g][:, t, :], op=ALU.add)
+            nc.sync.dma_start(out=out_groups[g][:, t, :], in_=gate[i][:])
+
+        def run(stage, i):
+            if 0 <= i < N_TILES:
+                stage(i)
+
+        for k in range(-3, N_TILES + 2):
+            first_of_next_group = k + 3 + GROUP_TILES
+            if first_of_next_group % GROUP_TILES == 0 and 2 * GROUP_TILES <= first_of_next_group < N_TILES:
+                load(first_of_next_group // GROUP_TILES)
+            run(quantise, k + 1)
+            run(matmuls, k + 1)
+            run(transposes, k + 3)
+            run(means, k)
+            run(copy_h, k + 2)
+            run(squares, k)
+            run(copy_x, k + 2)
+            run(add_hidden_norm, k - 1)
+            run(weigh_difference, k - 2)
+            run(add_input_norm, k - 1)
+            run(add_state_and_store, k - 2)
+            run(sigmoid, k - 1)
+            run(centre, k)
+            run(inverse_deviation, k)
+            run(difference, k)

@@ -39,7 +39,7 @@ def tile_layernormgrucell_pb_t_kernel(
     with ExitStack() as ctx:
         const = ctx.enter_context(tc.tile_pool(name="const", bufs=1))
         x_pool = ctx.enter_context(tc.tile_pool(name="x_pool", bufs=3))
-        hc_pool = ctx.enter_context(tc.tile_pool(name="hc_pool", bufs=4))
+        hc_pool = ctx.enter_context(tc.tile_pool(name="hc_pool", bufs=5))
         quant = ctx.enter_context(tc.tile_pool(name="quant", bufs=2))
         unread = ctx.enter_context(tc.tile_pool(name="unread", bufs=4))
         small = ctx.enter_context(tc.tile_pool(name="small", bufs=3))
@@ -183,7 +183,7 @@ def tile_layernormgrucell_pb_t_kernel(
 
         def centre(i):
             hid[i] = work.tile([P, H], F32, name="hid")
-            gate[i] = work.tile([P, H], F32, name="gate")
+            gate[i] = work.tile([P, H], F32, name="gate", bufs=6)
             for col, (acc, dst) in enumerate(((acc_h[i], hid[i]), (acc_x[i], gate[i]))):
                 nc.vector.scalar_tensor_tensor(
                     out=dst[:],
@@ -232,22 +232,22 @@ def tile_layernormgrucell_pb_t_kernel(
             if 0 <= i < N_TILES:
                 stage(i)
 
-        for k in range(-3, N_TILES + 2):
-            first_of_next_group = k + 3 + GROUP_TILES
+        for k in range(-4, N_TILES + 4):
+            first_of_next_group = k + 4 + GROUP_TILES
             if first_of_next_group % GROUP_TILES == 0 and 2 * GROUP_TILES <= first_of_next_group < N_TILES:
                 load(first_of_next_group // GROUP_TILES)
-            run(quantise, k + 1)
+            run(sigmoid, k - 3)
             run(matmuls, k + 1)
-            run(transposes, k + 3)
+            run(transposes, k + 4)
+            run(quantise, k + 2)
             run(means, k)
-            run(copy_h, k + 2)
+            run(copy_h, k + 3)
             run(squares, k)
-            run(copy_x, k + 2)
-            run(add_hidden_norm, k - 1)
-            run(weigh_difference, k - 2)
-            run(add_input_norm, k - 1)
-            run(add_state_and_store, k - 2)
-            run(sigmoid, k - 1)
+            run(copy_x, k + 3)
+            run(add_hidden_norm, k - 2)
+            run(weigh_difference, k - 4)
+            run(add_input_norm, k - 2)
+            run(add_state_and_store, k - 4)
             run(centre, k)
             run(inverse_deviation, k)
-            run(difference, k)
+            run(difference, k - 2)

@@ -39,7 +39,7 @@ def tile_layernormgrucell_pb_t_kernel(
     with ExitStack() as ctx:
         const = ctx.enter_context(tc.tile_pool(name="const", bufs=1))
         x_pool = ctx.enter_context(tc.tile_pool(name="x_pool", bufs=3))
-        hc_pool = ctx.enter_context(tc.tile_pool(name="hc_pool", bufs=5))
+        hc_pool = ctx.enter_context(tc.tile_pool(name="hc_pool", bufs=4))
         quant = ctx.enter_context(tc.tile_pool(name="quant", bufs=2))
         unread = ctx.enter_context(tc.tile_pool(name="unread", bufs=4))
         small = ctx.enter_context(tc.tile_pool(name="small", bufs=3))
@@ -183,7 +183,7 @@ def tile_layernormgrucell_pb_t_kernel(
 
         def centre(i):
             hid[i] = work.tile([P, H], F32, name="hid")
-            gate[i] = work.tile([P, H], F32, name="gate", bufs=6)
+            gate[i] = work.tile([P, H], F32, name="gate")
             for col, (acc, dst) in enumerate(((acc_h[i], hid[i]), (acc_x[i], gate[i]))):
                 nc.vector.scalar_tensor_tensor(
                     out=dst[:],
@@ -205,7 +205,7 @@ def tile_layernormgrucell_pb_t_kernel(
         def difference(i):
             g, t = divmod(i, GROUP_TILES)
             diff[i] = work.tile([P, H], F32, name="diff")
-            nc.gpsimd.tensor_tensor(out=diff[i][:], in0=c_sb[g][:, t, :], in1=h_sb[g][:, t, :], op=ALU.subtract)
+            nc.vector.tensor_tensor(out=diff[i][:], in0=c_sb[g][:, t, :], in1=h_sb[g][:, t, :], op=ALU.subtract)
 
         def add_hidden_norm(i):
             nc.vector.scalar_tensor_tensor(
@@ -232,22 +232,22 @@ def tile_layernormgrucell_pb_t_kernel(
             if 0 <= i < N_TILES:
                 stage(i)
 
-        for k in range(-4, N_TILES + 4):
-            first_of_next_group = k + 4 + GROUP_TILES
+        for k in range(-3, N_TILES + 2):
+            first_of_next_group = k + 3 + GROUP_TILES
             if first_of_next_group % GROUP_TILES == 0 and 2 * GROUP_TILES <= first_of_next_group < N_TILES:
                 load(first_of_next_group // GROUP_TILES)
-            run(sigmoid, k - 3)
+            run(quantise, k + 1)
+            run(difference, k)
             run(matmuls, k + 1)
-            run(transposes, k + 4)
-            run(quantise, k + 2)
+            run(transposes, k + 3)
             run(means, k)
-            run(copy_h, k + 3)
+            run(copy_h, k + 2)
             run(squares, k)
-            run(copy_x, k + 3)
-            run(add_hidden_norm, k - 2)
-            run(weigh_difference, k - 4)
-            run(add_input_norm, k - 2)
-            run(add_state_and_store, k - 4)
+            run(copy_x, k + 2)
+            run(add_hidden_norm, k - 1)
+            run(weigh_difference, k - 2)
+            run(add_input_norm, k - 1)
+            run(add_state_and_store, k - 2)
+            run(sigmoid, k - 1)
             run(centre, k)
             run(inverse_deviation, k)
-            run(difference, k - 2)

@@ -22,6 +22,7 @@ WORDS = K_PASS // 2
 GROUP_TILES = 4
 N_GROUPS = ROWS // (P * GROUP_TILES)
 N_TILES = ROWS // P
+VECTOR_DIFF_TILES = 13
 
 FLOPS = 2 * ROWS * H * (H + IN)
 
@@ -63,6 +64,10 @@ def tile_layernormgrucell_pb_t_kernel(
         nc.vector.memset(neg_half[:], -0.5)
         ident = const.tile([P, P], F32)
         masks.make_identity(nc, ident[:])
+        ident_bf = const.tile([P, P], BF16)
+        nc.vector.tensor_copy(out=ident_bf[:], in_=ident[:])
+        neg_ident_bf = const.tile([P, P], BF16)
+        nc.vector.tensor_scalar(out=neg_ident_bf[:], in0=ident[:], scalar1=-1.0, scalar2=None, op0=ALU.mult)
 
         load(0)
         w_words = const.tile([P, 1 + X_PASSES, 2 * H], U8, align_bytes=64)
@@ -104,8 +109,8 @@ def tile_layernormgrucell_pb_t_kernel(
             g, t = divmod(i, GROUP_TILES)
             x_words = x_sb[g][:, t, :].bitcast(F32)
             h_words = h_sb[g][:, t, :].bitcast(F32)
-            xT[i] = psum.tile([P, X_PASSES, 2, P], F32, name="xT")
-            hT[i] = psum.tile([P, 2, P], F32, name="hT")
+            hT[i] = psum.tile([P, 2, P], F32, name="hT", tag="words", bufs=3)
+            xT[i] = psum.tile([P, X_PASSES, 2, P], F32, name="xT", tag="words", bufs=3)
             for u in range(2):
                 nc.tensor.transpose(hT[i][:, u, :], h_words[:, u:WORDS:2], ident[:])
             for s in range(X_PASSES):
@@ -202,10 +207,20 @@ def tile_layernormgrucell_pb_t_kernel(
             rstd[i] = small.tile([P, 2], F32, name="rstd")
             nc.gpsimd.tensor_tensor(out=rstd[i][:], in0=var_eps[:], in1=neg_half[:], op=ALU.pow)
 
-        def difference(i):
+        def vector_difference(i):
+            if i >= VECTOR_DIFF_TILES:
+                return
             g, t = divmod(i, GROUP_TILES)
             diff[i] = work.tile([P, H], F32, name="diff")
             nc.vector.tensor_tensor(out=diff[i][:], in0=c_sb[g][:, t, :], in1=h_sb[g][:, t, :], op=ALU.subtract)
+
+        def tensor_difference(i):
+            if i < VECTOR_DIFF_TILES:
+                return
+            g, t = divmod(i, GROUP_TILES)
+            diff[i] = psum.tile([P, H], F32, name="diff_psum", bufs=1)
+            nc.tensor.matmul(diff[i][:], lhsT=ident_bf[:], rhs=c_sb[g][:, t, :], start=True, stop=False)
+            nc.tensor.matmul(diff[i][:], lhsT=neg_ident_bf[:], rhs=h_sb[g][:, t, :], start=False, stop=True)
 
         def add_hidden_norm(i):
             nc.vector.scalar_tensor_tensor(
@@ -237,15 +252,16 @@ def tile_layernormgrucell_pb_t_kernel(
             if first_of_next_group % GROUP_TILES == 0 and 2 * GROUP_TILES <= first_of_next_group < N_TILES:
                 load(first_of_next_group // GROUP_TILES)
             run(quantise, k + 1)
-            run(difference, k)
+            run(vector_difference, k)
             run(matmuls, k + 1)
-            run(transposes, k + 3)
             run(means, k)
             run(copy_h, k + 2)
             run(squares, k)
             run(copy_x, k + 2)
+            run(transposes, k + 3)
             run(add_hidden_norm, k - 1)
             run(weigh_difference, k - 2)
+            run(tensor_difference, k - 1)
             run(add_input_norm, k - 1)
             run(add_state_and_store, k - 2)
             run(sigmoid, k - 1)

@@ -44,7 +44,7 @@ def tile_layernormgrucell_pb_t_kernel(
         quant = ctx.enter_context(tc.tile_pool(name="quant", bufs=2))
         unread = ctx.enter_context(tc.tile_pool(name="unread", bufs=4))
         small = ctx.enter_context(tc.tile_pool(name="small", bufs=3))
-        work = ctx.enter_context(tc.tile_pool(name="work", bufs=4))
+        work = ctx.enter_context(tc.tile_pool(name="work", bufs=6))
         psum = ctx.enter_context(tc.psum_pool(name="psum", bufs=2))
         ctx.enter_context(tc.manual_schedule())
 
@@ -60,7 +60,7 @@ def tile_layernormgrucell_pb_t_kernel(
 
         w_scales = const.tile([P, 1 + X_PASSES, H], U8, align_bytes=64)
         nc.vector.memset(w_scales[:].rearrange("p w n -> p (w n)").bitcast(I32), 0)
-        neg_half = const.tile([P, 2], F32)
+        neg_half = const.tile([P, 4], F32)
         nc.vector.memset(neg_half[:], -0.5)
         ident = const.tile([P, P], F32)
         masks.make_identity(nc, ident[:])
@@ -102,15 +102,16 @@ def tile_layernormgrucell_pb_t_kernel(
         x_grouped, h_grouped = {}, {}
         x_codes, x_scales, h_codes, h_scales = {}, {}, {}, {}
         acc_h, acc_x = {}, {}
-        neg_mean, sq_sum, rstd = {}, {}, {}
+        folded = {}
+        neg_mean, sq_pair, sq_sum, rstd = {}, {}, {}, {}
         hid, gate, diff = {}, {}, {}
 
         def transposes(i):
             g, t = divmod(i, GROUP_TILES)
             x_words = x_sb[g][:, t, :].bitcast(F32)
             h_words = h_sb[g][:, t, :].bitcast(F32)
-            hT[i] = psum.tile([P, 2, P], F32, name="hT", tag="words", bufs=3)
-            xT[i] = psum.tile([P, X_PASSES, 2, P], F32, name="xT", tag="words", bufs=3)
+            hT[i] = psum.tile([P, 2, P], F32, name="hT", tag="words", bufs=2)
+            xT[i] = psum.tile([P, X_PASSES, 2, P], F32, name="xT", tag="words", bufs=2)
             for u in range(2):
                 nc.tensor.transpose(hT[i][:, u, :], h_words[:, u:WORDS:2], ident[:])
             for s in range(X_PASSES):
@@ -133,10 +134,12 @@ def tile_layernormgrucell_pb_t_kernel(
                 in_=xT[i][:].rearrange("p s u r -> p s r u"),
             )
 
-        def quantise(i):
+        def quantise_h(i):
             h_codes[i] = quant.tile([P, P], U32, name="h_codes", align_bytes=64)
             h_scales[i] = quant.tile([P, P], U8, name="h_scales", align_bytes=64)
             nc.vector.quantize_mx(out=h_codes[i][:].bitcast(FP8X4), scales=h_scales[i][:], in_=h_grouped[i][:])
+
+        def quantise_x(i):
             x_codes[i] = quant.tile([P, X_PASSES * P], U32, name="x_codes", align_bytes=64)
             x_scales[i] = quant.tile([P, X_PASSES * P], U8, name="x_scales", align_bytes=64)
             nc.vector.quantize_mx(out=x_codes[i][:].bitcast(FP8X4), scales=x_scales[i][:], in_=x_grouped[i][:])
@@ -165,16 +168,38 @@ def tile_layernormgrucell_pb_t_kernel(
                     stop=(s == X_PASSES - 1),
                 )
 
+        def folded_matmuls(i):
+            folded[i] = psum.tile([P, 2, P], F32, name="folded", bufs=1)
+            for col, codes, scales, weights in ((0, h_codes[i], h_scales[i], (0,)), (1, x_codes[i], x_scales[i], (1, 2))):
+                passes = [(s, w, q) for s, w in enumerate(weights) for q in range(H // P)]
+                for j, (s, w, q) in enumerate(passes):
+                    rows = slice(s * P, (s + 1) * P)
+                    nc.tensor.matmul_mx(
+                        out=folded[i][:, col, :],
+                        lhsT=codes[:, rows].bitcast(FP8X4),
+                        lhsT_scale=scales[:, rows],
+                        rhs=w_words[:, w, 2 * q * P : 2 * (q + 1) * P].bitcast(FP4X4),
+                        rhs_scale=w_scales[:, w, q * P : (q + 1) * P],
+                        start=(j == 0),
+                        stop=(j == len(passes) - 1),
+                    )
+
         def means(i):
-            sums = small.tile([P, 2], F32, name="sums")
-            for col, acc in enumerate((acc_h[i], acc_x[i])):
-                scrap = unread.tile([P, H], F32, name="scrap")
-                nc.scalar.activation(out=scrap[:], in_=acc[:], func=ACT.Identity, accum_out=sums[:, col : col + 1])
             neg_mean[i] = small.tile([P, 2], F32, name="neg_mean")
-            nc.scalar.mul(out=neg_mean[i][:], in_=sums[:], mul=-1.0 / H)
+            for col in range(2):
+                scrap = unread.tile([P, P], F32, name="mean_scrap")
+                nc.scalar.activation(
+                    out=scrap[:],
+                    in_=folded[i][:, col, :],
+                    func=ACT.Identity,
+                    scale=-1.0 / H,
+                    accum_out=neg_mean[i][:, col : col + 1],
+                )
 
         def squares(i):
-            sq_sum[i] = small.tile([P, 2], F32, name="sq_sum")
+            if i % 2 == 0:
+                sq_pair[i // 2] = small.tile([P, 2, 2], F32, name="sq_sum")
+            sq_sum[i] = sq_pair[i // 2][:, i % 2, :]
             for col, acc in enumerate((acc_h[i], acc_x[i])):
                 scrap = unread.tile([P, H], F32, name="scrap")
                 nc.scalar.activation(
@@ -186,26 +211,39 @@ def tile_layernormgrucell_pb_t_kernel(
                     accum_out=sq_sum[i][:, col : col + 1],
                 )
 
-        def centre(i):
-            hid[i] = work.tile([P, H], F32, name="hid")
-            gate[i] = work.tile([P, H], F32, name="gate")
-            for col, (acc, dst) in enumerate(((acc_h[i], hid[i]), (acc_x[i], gate[i]))):
-                nc.vector.scalar_tensor_tensor(
-                    out=dst[:],
-                    in0=acc[:],
-                    scalar=neg_mean[i][:, col : col + 1],
-                    in1=gamma[:, col, :],
-                    op0=ALU.add,
-                    op1=ALU.mult,
-                )
-
-        def inverse_deviation(i):
-            var_eps = small.tile([P, 2], F32, name="var_eps")
-            nc.gpsimd.tensor_scalar(
-                out=var_eps[:], in0=sq_sum[i][:], scalar1=1.0 / H, scalar2=EPS, op0=ALU.mult, op1=ALU.add
+        def centre(i, col, acc, dst):
+            nc.vector.scalar_tensor_tensor(
+                out=dst[:],
+                in0=acc[:],
+                scalar=neg_mean[i][:, col : col + 1],
+                in1=gamma[:, col, :],
+                op0=ALU.add,
+                op1=ALU.mult,
             )
-            rstd[i] = small.tile([P, 2], F32, name="rstd")
-            nc.gpsimd.tensor_tensor(out=rstd[i][:], in0=var_eps[:], in1=neg_half[:], op=ALU.pow)
+
+        def centre_h(i):
+            hid[i] = work.tile([P, H], F32, name="hid")
+            centre(i, 0, acc_h[i], hid[i])
+
+        def centre_x(i):
+            gate[i] = work.tile([P, H], F32, name="gate")
+            centre(i, 1, acc_x[i], gate[i])
+
+        def inverse_deviations(i):
+            if i % 2 == 0:
+                return
+            var_eps = small.tile([P, 4], F32, name="var_eps")
+            nc.gpsimd.tensor_scalar(
+                out=var_eps[:],
+                in0=sq_pair[i // 2][:].rearrange("p i n -> p (i n)"),
+                scalar1=1.0 / H,
+                scalar2=EPS,
+                op0=ALU.mult,
+                op1=ALU.add,
+            )
+            rstd_pair = small.tile([P, 4], F32, name="rstd")
+            nc.gpsimd.tensor_tensor(out=rstd_pair[:], in0=var_eps[:], in1=neg_half[:], op=ALU.pow)
+            rstd[i - 1], rstd[i] = rstd_pair[:, 0:2], rstd_pair[:, 2:4]
 
         def vector_difference(i):
             if i >= VECTOR_DIFF_TILES:
@@ -240,30 +278,33 @@ def tile_layernormgrucell_pb_t_kernel(
 
         def add_state_and_store(i):
             g, t = divmod(i, GROUP_TILES)
-            nc.vector.tensor_tensor(out=gate[i][:], in0=gate[i][:], in1=h_sb[g][:, t, :], op=ALU.add)
+            nc.gpsimd.tensor_tensor(out=gate[i][:], in0=gate[i][:], in1=h_sb[g][:, t, :], op=ALU.add)
             nc.sync.dma_start(out=out_groups[g][:, t, :], in_=gate[i][:])
 
         def run(stage, i):
             if 0 <= i < N_TILES:
                 stage(i)
 
-        for k in range(-3, N_TILES + 2):
+        for k in range(-3, N_TILES + 3):
             first_of_next_group = k + 3 + GROUP_TILES
             if first_of_next_group % GROUP_TILES == 0 and 2 * GROUP_TILES <= first_of_next_group < N_TILES:
                 load(first_of_next_group // GROUP_TILES)
-            run(quantise, k + 1)
-            run(vector_difference, k)
+            run(weigh_difference, k - 3)
             run(matmuls, k + 1)
-            run(means, k)
+            run(folded_matmuls, k + 1)
             run(copy_h, k + 2)
-            run(squares, k)
             run(copy_x, k + 2)
-            run(transposes, k + 3)
+            run(sigmoid, k - 2)
+            run(centre_h, k)
+            run(add_state_and_store, k - 3)
+            run(centre_x, k)
             run(add_hidden_norm, k - 1)
-            run(weigh_difference, k - 2)
-            run(tensor_difference, k - 1)
+            run(quantise_h, k + 2)
+            run(quantise_x, k + 2)
             run(add_input_norm, k - 1)
-            run(add_state_and_store, k - 2)
-            run(sigmoid, k - 1)
-            run(centre, k)
-            run(inverse_deviation, k)
+            run(vector_difference, k)
+            run(transposes, k + 3)
+            run(tensor_difference, k - 2)
+            run(means, k + 1)
+            run(squares, k + 1)
+            run(inverse_deviations, k + 1)

@@ -22,7 +22,8 @@ WORDS = K_PASS // 2
 GROUP_TILES = 4
 N_GROUPS = ROWS // (P * GROUP_TILES)
 N_TILES = ROWS // P
-VECTOR_DIFF_TILES = 13
+VECTOR_DIFF_TILES = 14
+GPSIMD_ADD_TILES = N_TILES - 2
 
 FLOPS = 2 * ROWS * H * (H + IN)
 
@@ -44,7 +45,7 @@ def tile_layernormgrucell_pb_t_kernel(
         quant = ctx.enter_context(tc.tile_pool(name="quant", bufs=2))
         unread = ctx.enter_context(tc.tile_pool(name="unread", bufs=4))
         small = ctx.enter_context(tc.tile_pool(name="small", bufs=3))
-        work = ctx.enter_context(tc.tile_pool(name="work", bufs=6))
+        work = ctx.enter_context(tc.tile_pool(name="work", bufs=8))
         psum = ctx.enter_context(tc.psum_pool(name="psum", bufs=2))
         ctx.enter_context(tc.manual_schedule())
 
@@ -69,7 +70,11 @@ def tile_layernormgrucell_pb_t_kernel(
         neg_ident_bf = const.tile([P, P], BF16)
         nc.vector.tensor_scalar(out=neg_ident_bf[:], in0=ident[:], scalar1=-1.0, scalar2=None, op0=ALU.mult)
 
-        load(0)
+        x_sb[0] = x_pool.tile([P, GROUP_TILES, IN], BF16, name="x_rows")
+        h_sb[0] = hc_pool.tile([P, GROUP_TILES, H], BF16, name="h_rows")
+        c_sb[0] = hc_pool.tile([P, GROUP_TILES, H], BF16, name="c_rows")
+        nc.sync.dma_start(out=h_sb[0][:, 0, :], in_=h_groups[0][:, 0, :])
+        nc.sync.dma_start(out=x_sb[0][:, 0, :], in_=x_groups[0][:, 0, :])
         w_words = const.tile([P, 1 + X_PASSES, 2 * H], U8, align_bytes=64)
         for q in range(4):
             nc.sync.dma_start(
@@ -89,31 +94,40 @@ def tile_layernormgrucell_pb_t_kernel(
             out=gamma[:].rearrange("p i n -> p (i n)"),
             in_=ln_gamma.rearrange("i n -> (i n)").partition_broadcast(P),
         )
-        beta = const.tile([P, 2, H], BF16)
-        nc.sync.dma_start(
-            out=beta[:].rearrange("p i n -> p (i n)"),
-            in_=ln_beta.rearrange("i n -> (i n)").partition_broadcast(P),
-        )
-        beta_sum = const.tile([P, H], F32)
-        nc.gpsimd.tensor_tensor(out=beta_sum[:], in0=beta[:, 0, :], in1=beta[:, 1, :], op=ALU.add)
+        beta_rows = const.tile([P, H], BF16)
+        nc.gpsimd.memset(beta_rows[:], 0.0)
+        ones = const.tile([P, P], BF16)
+        nc.gpsimd.memset(ones[:], 1.0)
+        nc.sync.dma_start(out=beta_rows[0:2, :], in_=ln_beta)
+        beta_sum = psum.tile([P, H], F32, name="beta_sum", bufs=1)
+        nc.sync.dma_start(out=h_sb[0][:, 1:, :], in_=h_groups[0][:, 1:, :])
+        nc.sync.dma_start(out=c_sb[0][:], in_=c_groups[0])
+        nc.sync.dma_start(out=x_sb[0][:, 1:, :], in_=x_groups[0][:, 1:, :])
         load(1)
 
-        xT, hT = {}, {}
+        xT = {}
         x_grouped, h_grouped = {}, {}
         x_codes, x_scales, h_codes, h_scales = {}, {}, {}, {}
         acc_h, acc_x = {}, {}
-        folded = {}
         neg_mean, sq_pair, sq_sum, rstd = {}, {}, {}, {}
         hid, gate, diff = {}, {}, {}
 
-        def transposes(i):
+        shared_bank = psum.tile([P, 4, P], F32, name="shared_bank", bufs=1)
+        h_words_bank, folded = shared_bank[:, 0:2, :], shared_bank[:, 2:4, :]
+
+        def spread_beta():
+            nc.tensor.matmul(beta_sum[:], lhsT=ones[:], rhs=beta_rows[:], start=True, stop=True)
+
+        def transposes_h(i):
+            g, t = divmod(i, GROUP_TILES)
+            h_words = h_sb[g][:, t, :].bitcast(F32)
+            for u in range(2):
+                nc.tensor.transpose(h_words_bank[:, u, :], h_words[:, u:WORDS:2], ident[:])
+
+        def transposes_x(i):
             g, t = divmod(i, GROUP_TILES)
             x_words = x_sb[g][:, t, :].bitcast(F32)
-            h_words = h_sb[g][:, t, :].bitcast(F32)
-            hT[i] = psum.tile([P, 2, P], F32, name="hT", tag="words", bufs=2)
-            xT[i] = psum.tile([P, X_PASSES, 2, P], F32, name="xT", tag="words", bufs=2)
-            for u in range(2):
-                nc.tensor.transpose(hT[i][:, u, :], h_words[:, u:WORDS:2], ident[:])
+            xT[i] = psum.tile([P, X_PASSES, 2, P], F32, name="xT", bufs=1)
             for s in range(X_PASSES):
                 for u in range(2):
                     nc.tensor.transpose(
@@ -124,7 +138,7 @@ def tile_layernormgrucell_pb_t_kernel(
             h_grouped[i] = quant.tile([P, 4 * P], BF16, name="h_grouped", align_bytes=64)
             nc.scalar.copy(
                 out=h_grouped[i][:].bitcast(F32).rearrange("p (r u) -> p r u", u=2),
-                in_=hT[i][:].rearrange("p u r -> p r u"),
+                in_=h_words_bank.rearrange("p u r -> p r u"),
             )
 
         def copy_x(i):
@@ -169,13 +183,12 @@ def tile_layernormgrucell_pb_t_kernel(
                 )
 
         def folded_matmuls(i):
-            folded[i] = psum.tile([P, 2, P], F32, name="folded", bufs=1)
             for col, codes, scales, weights in ((0, h_codes[i], h_scales[i], (0,)), (1, x_codes[i], x_scales[i], (1, 2))):
                 passes = [(s, w, q) for s, w in enumerate(weights) for q in range(H // P)]
                 for j, (s, w, q) in enumerate(passes):
                     rows = slice(s * P, (s + 1) * P)
                     nc.tensor.matmul_mx(
-                        out=folded[i][:, col, :],
+                        out=folded[:, col, :],
                         lhsT=codes[:, rows].bitcast(FP8X4),
                         lhsT_scale=scales[:, rows],
                         rhs=w_words[:, w, 2 * q * P : 2 * (q + 1) * P].bitcast(FP4X4),
@@ -190,7 +203,7 @@ def tile_layernormgrucell_pb_t_kernel(
                 scrap = unread.tile([P, P], F32, name="mean_scrap")
                 nc.scalar.activation(
                     out=scrap[:],
-                    in_=folded[i][:, col, :],
+                    in_=folded[:, col, :],
                     func=ACT.Identity,
                     scale=-1.0 / H,
                     accum_out=neg_mean[i][:, col : col + 1],
@@ -278,33 +291,41 @@ def tile_layernormgrucell_pb_t_kernel(
 
         def add_state_and_store(i):
             g, t = divmod(i, GROUP_TILES)
-            nc.gpsimd.tensor_tensor(out=gate[i][:], in0=gate[i][:], in1=h_sb[g][:, t, :], op=ALU.add)
+            adder = nc.gpsimd if i < GPSIMD_ADD_TILES else nc.vector
+            adder.tensor_tensor(out=gate[i][:], in0=gate[i][:], in1=h_sb[g][:, t, :], op=ALU.add)
             nc.sync.dma_start(out=out_groups[g][:, t, :], in_=gate[i][:])
 
         def run(stage, i):
             if 0 <= i < N_TILES:
                 stage(i)
 
-        for k in range(-3, N_TILES + 3):
+        for k in range(-3, N_TILES + 4):
             first_of_next_group = k + 3 + GROUP_TILES
             if first_of_next_group % GROUP_TILES == 0 and 2 * GROUP_TILES <= first_of_next_group < N_TILES:
                 load(first_of_next_group // GROUP_TILES)
-            run(weigh_difference, k - 3)
+            run(weigh_difference, k - 4)
+            run(add_state_and_store, k - 4)
+            run(inverse_deviations, k)
             run(matmuls, k + 1)
-            run(folded_matmuls, k + 1)
             run(copy_h, k + 2)
             run(copy_x, k + 2)
-            run(sigmoid, k - 2)
+            run(folded_matmuls, k + 1)
+            run(sigmoid, k - 3)
             run(centre_h, k)
-            run(add_state_and_store, k - 3)
             run(centre_x, k)
-            run(add_hidden_norm, k - 1)
+            run(add_hidden_norm, k - 2)
             run(quantise_h, k + 2)
             run(quantise_x, k + 2)
-            run(add_input_norm, k - 1)
-            run(vector_difference, k)
-            run(transposes, k + 3)
-            run(tensor_difference, k - 2)
+            if k == -1:
+                for i in range(GROUP_TILES):
+                    vector_difference(i)
+            if k >= GROUP_TILES:
+                run(vector_difference, k)
+            run(add_input_norm, k - 2)
+            run(transposes_x, k + 3)
+            if k == -1:
+                spread_beta()
+            run(tensor_difference, k - 3)
             run(means, k + 1)
+            run(transposes_h, k + 3)
             run(squares, k + 1)
-            run(inverse_deviations, k + 1)

@@ -42,9 +42,9 @@ def tile_layernormgrucell_pb_t_kernel(
         const = ctx.enter_context(tc.tile_pool(name="const", bufs=1))
         x_pool = ctx.enter_context(tc.tile_pool(name="x_pool", bufs=3))
         hc_pool = ctx.enter_context(tc.tile_pool(name="hc_pool", bufs=4))
-        quant = ctx.enter_context(tc.tile_pool(name="quant", bufs=2))
+        quant = ctx.enter_context(tc.tile_pool(name="quant", bufs=3))
         unread = ctx.enter_context(tc.tile_pool(name="unread", bufs=4))
-        small = ctx.enter_context(tc.tile_pool(name="small", bufs=3))
+        small = ctx.enter_context(tc.tile_pool(name="small", bufs=4))
         work = ctx.enter_context(tc.tile_pool(name="work", bufs=8))
         psum = ctx.enter_context(tc.psum_pool(name="psum", bufs=2))
         ctx.enter_context(tc.manual_schedule())
@@ -73,8 +73,12 @@ def tile_layernormgrucell_pb_t_kernel(
         x_sb[0] = x_pool.tile([P, GROUP_TILES, IN], BF16, name="x_rows")
         h_sb[0] = hc_pool.tile([P, GROUP_TILES, H], BF16, name="h_rows")
         c_sb[0] = hc_pool.tile([P, GROUP_TILES, H], BF16, name="c_rows")
-        nc.sync.dma_start(out=h_sb[0][:, 0, :], in_=h_groups[0][:, 0, :])
-        nc.sync.dma_start(out=x_sb[0][:, 0, :], in_=x_groups[0][:, 0, :])
+
+        def load_first(tiles):
+            nc.sync.dma_start(out=h_sb[0][:, tiles, :], in_=h_groups[0][:, tiles, :])
+            nc.sync.dma_start(out=x_sb[0][:, tiles, :], in_=x_groups[0][:, tiles, :])
+
+        load_first(slice(0, 1))
         w_words = const.tile([P, 1 + X_PASSES, 2 * H], U8, align_bytes=64)
         for q in range(4):
             nc.sync.dma_start(
@@ -82,6 +86,7 @@ def tile_layernormgrucell_pb_t_kernel(
                 in_=W_u_scales[0, 4 * q : 4 * q + 4, :].bitcast(I32),
             )
         nc.sync.dma_start(out=w_words[:, 0, :].bitcast(I32), in_=W_u_words[0].bitcast(I32))
+        load_first(slice(1, 2))
         for q in range(4):
             nc.sync.dma_start(
                 out=w_scales[32 * q : 32 * q + 4, 1:, :].bitcast(I32),
@@ -100,9 +105,8 @@ def tile_layernormgrucell_pb_t_kernel(
         nc.gpsimd.memset(ones[:], 1.0)
         nc.sync.dma_start(out=beta_rows[0:2, :], in_=ln_beta)
         beta_sum = psum.tile([P, H], F32, name="beta_sum", bufs=1)
-        nc.sync.dma_start(out=h_sb[0][:, 1:, :], in_=h_groups[0][:, 1:, :])
+        load_first(slice(2, 4))
         nc.sync.dma_start(out=c_sb[0][:], in_=c_groups[0])
-        nc.sync.dma_start(out=x_sb[0][:, 1:, :], in_=x_groups[0][:, 1:, :])
         load(1)
 
         xT = {}
@@ -239,7 +243,7 @@ def tile_layernormgrucell_pb_t_kernel(
             centre(i, 0, acc_h[i], hid[i])
 
         def centre_x(i):
-            gate[i] = work.tile([P, H], F32, name="gate")
+            gate[i] = work.tile([P, H], F32, name="gate", bufs=10)
             centre(i, 1, acc_x[i], gate[i])
 
         def inverse_deviations(i):
@@ -262,7 +266,7 @@ def tile_layernormgrucell_pb_t_kernel(
             if i >= VECTOR_DIFF_TILES:
                 return
             g, t = divmod(i, GROUP_TILES)
-            diff[i] = work.tile([P, H], F32, name="diff")
+            diff[i] = work.tile([P, H], F32, name="diff", bufs=VECTOR_DIFF_TILES)
             nc.vector.tensor_tensor(out=diff[i][:], in0=c_sb[g][:, t, :], in1=h_sb[g][:, t, :], op=ALU.subtract)
 
         def tensor_difference(i):
@@ -291,41 +295,46 @@ def tile_layernormgrucell_pb_t_kernel(
 
         def add_state_and_store(i):
             g, t = divmod(i, GROUP_TILES)
-            adder = nc.gpsimd if i < GPSIMD_ADD_TILES else nc.vector
-            adder.tensor_tensor(out=gate[i][:], in0=gate[i][:], in1=h_sb[g][:, t, :], op=ALU.add)
-            nc.sync.dma_start(out=out_groups[g][:, t, :], in_=gate[i][:])
+            if i < GPSIMD_ADD_TILES:
+                adder, total = nc.gpsimd, hid[i + 1]
+            else:
+                adder, total = nc.vector, gate[i]
+            adder.tensor_tensor(out=total[:], in0=gate[i][:], in1=h_sb[g][:, t, :], op=ALU.add)
+            nc.sync.dma_start(out=out_groups[g][:, t, :], in_=total[:])
 
         def run(stage, i):
             if 0 <= i < N_TILES:
                 stage(i)
 
+        early_diffs = {0: range(0, 3), 1: range(3, 6), 2: range(6, 8)}
         for k in range(-3, N_TILES + 4):
             first_of_next_group = k + 3 + GROUP_TILES
             if first_of_next_group % GROUP_TILES == 0 and 2 * GROUP_TILES <= first_of_next_group < N_TILES:
                 load(first_of_next_group // GROUP_TILES)
-            run(weigh_difference, k - 4)
-            run(add_state_and_store, k - 4)
-            run(inverse_deviations, k)
-            run(matmuls, k + 1)
-            run(copy_h, k + 2)
-            run(copy_x, k + 2)
-            run(folded_matmuls, k + 1)
-            run(sigmoid, k - 3)
-            run(centre_h, k)
-            run(centre_x, k)
             run(add_hidden_norm, k - 2)
-            run(quantise_h, k + 2)
-            run(quantise_x, k + 2)
-            if k == -1:
-                for i in range(GROUP_TILES):
-                    vector_difference(i)
-            if k >= GROUP_TILES:
-                run(vector_difference, k)
-            run(add_input_norm, k - 2)
-            run(transposes_x, k + 3)
+            run(folded_matmuls, k + 1)
+            run(matmuls, k + 1)
             if k == -1:
                 spread_beta()
-            run(tensor_difference, k - 3)
+            run(sigmoid, k - 3)
+            run(copy_x, k + 2)
+            run(centre_h, k)
+            run(centre_x, k)
+            run(weigh_difference, k - 3)
+            run(quantise_h, k + 2)
+            run(quantise_x, k + 2)
+            for i in early_diffs.get(k, range(k + 5, k + 6)):
+                if k >= 0:
+                    run(vector_difference, i)
+            if k - 4 >= GPSIMD_ADD_TILES:
+                run(add_state_and_store, k - 4)
+            run(add_input_norm, k - 2)
+            run(inverse_deviations, k)
+            if k - 3 < GPSIMD_ADD_TILES:
+                run(add_state_and_store, k - 3)
             run(means, k + 1)
             run(transposes_h, k + 3)
+            run(transposes_x, k + 3)
+            run(tensor_difference, k - 2)
             run(squares, k + 1)
+            run(copy_h, k + 3)

@@ -22,8 +22,7 @@ WORDS = K_PASS // 2
 GROUP_TILES = 4
 N_GROUPS = ROWS // (P * GROUP_TILES)
 N_TILES = ROWS // P
-VECTOR_DIFF_TILES = 14
-GPSIMD_ADD_TILES = N_TILES - 2
+VECTOR_DIFF_TILES = 13
 
 FLOPS = 2 * ROWS * H * (H + IN)
 
@@ -99,13 +98,14 @@ def tile_layernormgrucell_pb_t_kernel(
             out=gamma[:].rearrange("p i n -> p (i n)"),
             in_=ln_gamma.rearrange("i n -> (i n)").partition_broadcast(P),
         )
-        beta_rows = const.tile([P, H], BF16)
-        nc.gpsimd.memset(beta_rows[:], 0.0)
-        ones = const.tile([P, P], BF16)
-        nc.gpsimd.memset(ones[:], 1.0)
-        nc.sync.dma_start(out=beta_rows[0:2, :], in_=ln_beta)
-        beta_sum = psum.tile([P, H], F32, name="beta_sum", bufs=1)
         load_first(slice(2, 4))
+        beta = const.tile([P, 2, H], BF16)
+        nc.sync.dma_start(
+            out=beta[:].rearrange("p i n -> p (i n)"),
+            in_=ln_beta.rearrange("i n -> (i n)").partition_broadcast(P),
+        )
+        beta_sum = const.tile([P, H], F32)
+        nc.gpsimd.tensor_tensor(out=beta_sum[:], in0=beta[:, 0, :], in1=beta[:, 1, :], op=ALU.add)
         nc.sync.dma_start(out=c_sb[0][:], in_=c_groups[0])
         load(1)
 
@@ -115,12 +115,10 @@ def tile_layernormgrucell_pb_t_kernel(
         acc_h, acc_x = {}, {}
         neg_mean, sq_pair, sq_sum, rstd = {}, {}, {}, {}
         hid, gate, diff = {}, {}, {}
+        gate_pair, diff_pair = {}, {}
 
         shared_bank = psum.tile([P, 4, P], F32, name="shared_bank", bufs=1)
         h_words_bank, folded = shared_bank[:, 0:2, :], shared_bank[:, 2:4, :]
-
-        def spread_beta():
-            nc.tensor.matmul(beta_sum[:], lhsT=ones[:], rhs=beta_rows[:], start=True, stop=True)
 
         def transposes_h(i):
             g, t = divmod(i, GROUP_TILES)
@@ -230,7 +228,7 @@ def tile_layernormgrucell_pb_t_kernel(
 
         def centre(i, col, acc, dst):
             nc.vector.scalar_tensor_tensor(
-                out=dst[:],
+                out=dst,
                 in0=acc[:],
                 scalar=neg_mean[i][:, col : col + 1],
                 in1=gamma[:, col, :],
@@ -240,10 +238,12 @@ def tile_layernormgrucell_pb_t_kernel(
 
         def centre_h(i):
             hid[i] = work.tile([P, H], F32, name="hid")
-            centre(i, 0, acc_h[i], hid[i])
+            centre(i, 0, acc_h[i], hid[i][:])
 
         def centre_x(i):
-            gate[i] = work.tile([P, H], F32, name="gate", bufs=10)
+            if i % 2 == 0:
+                gate_pair[i // 2] = work.tile([P, 2, H], F32, name="gate", bufs=6)
+            gate[i] = gate_pair[i // 2][:, i % 2, :]
             centre(i, 1, acc_x[i], gate[i])
 
         def inverse_deviations(i):
@@ -262,20 +262,26 @@ def tile_layernormgrucell_pb_t_kernel(
             nc.gpsimd.tensor_tensor(out=rstd_pair[:], in0=var_eps[:], in1=neg_half[:], op=ALU.pow)
             rstd[i - 1], rstd[i] = rstd_pair[:, 0:2], rstd_pair[:, 2:4]
 
-        def vector_difference(i):
-            if i >= VECTOR_DIFF_TILES:
-                return
-            g, t = divmod(i, GROUP_TILES)
-            diff[i] = work.tile([P, H], F32, name="diff", bufs=VECTOR_DIFF_TILES)
-            nc.vector.tensor_tensor(out=diff[i][:], in0=c_sb[g][:, t, :], in1=h_sb[g][:, t, :], op=ALU.subtract)
+        def vector_differences(first, count):
+            g, t = divmod(first, GROUP_TILES)
+            wide = work.tile([P, count, H], F32, name="diff_%d" % first, bufs=1)
+            nc.vector.tensor_tensor(
+                out=wide[:],
+                in0=c_sb[g][:, t : t + count, :],
+                in1=h_sb[g][:, t : t + count, :],
+                op=ALU.subtract,
+            )
+            for j in range(count):
+                diff[first + j] = wide[:, j, :]
 
         def tensor_difference(i):
             if i < VECTOR_DIFF_TILES:
                 return
             g, t = divmod(i, GROUP_TILES)
-            diff[i] = psum.tile([P, H], F32, name="diff_psum", bufs=1)
-            nc.tensor.matmul(diff[i][:], lhsT=ident_bf[:], rhs=c_sb[g][:, t, :], start=True, stop=False)
-            nc.tensor.matmul(diff[i][:], lhsT=neg_ident_bf[:], rhs=h_sb[g][:, t, :], start=False, stop=True)
+            bank = psum.tile([P, H], F32, name="diff_psum", bufs=2)
+            diff[i] = bank[:]
+            nc.tensor.matmul(diff[i], lhsT=ident_bf[:], rhs=c_sb[g][:, t, :], start=True, stop=False)
+            nc.tensor.matmul(diff[i], lhsT=neg_ident_bf[:], rhs=h_sb[g][:, t, :], start=False, stop=True)
 
         def add_hidden_norm(i):
             nc.vector.scalar_tensor_tensor(
@@ -284,54 +290,47 @@ def tile_layernormgrucell_pb_t_kernel(
 
         def add_input_norm(i):
             nc.vector.scalar_tensor_tensor(
-                out=gate[i][:], in0=gate[i][:], scalar=rstd[i][:, 1:2], in1=hid[i][:], op0=ALU.mult, op1=ALU.add
+                out=gate[i], in0=gate[i], scalar=rstd[i][:, 1:2], in1=hid[i][:], op0=ALU.mult, op1=ALU.add
             )
 
         def sigmoid(i):
-            nc.scalar.activation(out=gate[i][:], in_=gate[i][:], func=ACT.Sigmoid)
+            nc.scalar.activation(out=gate[i], in_=gate[i], func=ACT.Sigmoid)
 
         def weigh_difference(i):
-            nc.vector.tensor_tensor(out=gate[i][:], in0=gate[i][:], in1=diff[i][:], op=ALU.mult)
+            nc.vector.tensor_tensor(out=gate[i], in0=gate[i], in1=diff[i], op=ALU.mult)
 
         def add_state_and_store(i):
+            if i % 2 == 1:
+                return
             g, t = divmod(i, GROUP_TILES)
-            if i < GPSIMD_ADD_TILES:
-                adder, total = nc.gpsimd, hid[i + 1]
-            else:
-                adder, total = nc.vector, gate[i]
-            adder.tensor_tensor(out=total[:], in0=gate[i][:], in1=h_sb[g][:, t, :], op=ALU.add)
-            nc.sync.dma_start(out=out_groups[g][:, t, :], in_=total[:])
+            pair = gate_pair[i // 2]
+            nc.vector.tensor_tensor(out=pair[:], in0=pair[:], in1=h_sb[g][:, t : t + 2, :], op=ALU.add)
+            nc.sync.dma_start(out=out_groups[g][:, t : t + 2, :], in_=pair[:])
 
         def run(stage, i):
             if 0 <= i < N_TILES:
                 stage(i)
 
-        early_diffs = {0: range(0, 3), 1: range(3, 6), 2: range(6, 8)}
-        for k in range(-3, N_TILES + 4):
+        early_diffs = {0: ((0, 2), (2, 1)), 1: ((3, 1), (4, 2)), 2: ((6, 2),), 3: ((8, 2),), 4: ((10, 2),), 5: ((12, 1),)}
+        for k in range(-3, N_TILES + 6):
             first_of_next_group = k + 3 + GROUP_TILES
             if first_of_next_group % GROUP_TILES == 0 and 2 * GROUP_TILES <= first_of_next_group < N_TILES:
                 load(first_of_next_group // GROUP_TILES)
             run(add_hidden_norm, k - 2)
             run(folded_matmuls, k + 1)
             run(matmuls, k + 1)
-            if k == -1:
-                spread_beta()
             run(sigmoid, k - 3)
             run(copy_x, k + 2)
             run(centre_h, k)
+            run(add_state_and_store, k - 5)
             run(centre_x, k)
-            run(weigh_difference, k - 3)
             run(quantise_h, k + 2)
+            run(weigh_difference, k - 3)
             run(quantise_x, k + 2)
-            for i in early_diffs.get(k, range(k + 5, k + 6)):
-                if k >= 0:
-                    run(vector_difference, i)
-            if k - 4 >= GPSIMD_ADD_TILES:
-                run(add_state_and_store, k - 4)
+            for first, count in early_diffs.get(k, ()):
+                vector_differences(first, count)
             run(add_input_norm, k - 2)
             run(inverse_deviations, k)
-            if k - 3 < GPSIMD_ADD_TILES:
-                run(add_state_and_store, k - 3)
             run(means, k + 1)
             run(transposes_h, k + 3)
             run(transposes_x, k + 3)

@@ -22,7 +22,7 @@ WORDS = K_PASS // 2
 GROUP_TILES = 4
 N_GROUPS = ROWS // (P * GROUP_TILES)
 N_TILES = ROWS // P
-VECTOR_DIFF_TILES = 13
+VECTOR_DIFF_TILES = 15
 
 FLOPS = 2 * ROWS * H * (H + IN)
 
@@ -64,6 +64,10 @@ def tile_layernormgrucell_pb_t_kernel(
         nc.vector.memset(neg_half[:], -0.5)
         ident = const.tile([P, P], F32)
         masks.make_identity(nc, ident[:])
+        rows = const.tile([P, 3, H], BF16)
+        nc.gpsimd.memset(rows[:], 0.0)
+        ones = const.tile([P, P], BF16)
+        nc.gpsimd.memset(ones[:], 1.0)
         ident_bf = const.tile([P, P], BF16)
         nc.vector.tensor_copy(out=ident_bf[:], in_=ident[:])
         neg_ident_bf = const.tile([P, P], BF16)
@@ -84,30 +88,28 @@ def tile_layernormgrucell_pb_t_kernel(
                 out=w_scales[32 * q : 32 * q + 4, 0, :].bitcast(I32),
                 in_=W_u_scales[0, 4 * q : 4 * q + 4, :].bitcast(I32),
             )
-        nc.sync.dma_start(out=w_words[:, 0, :].bitcast(I32), in_=W_u_words[0].bitcast(I32))
-        load_first(slice(1, 2))
         for q in range(4):
             nc.sync.dma_start(
                 out=w_scales[32 * q : 32 * q + 4, 1:, :].bitcast(I32),
                 in_=U_u_scales[:, 4 * q : 4 * q + 4, :].rearrange("g r n -> r g n").bitcast(I32),
             )
+        nc.sync.dma_start(out=w_words[:, 0, :].bitcast(I32), in_=W_u_words[0].bitcast(I32))
         for g in range(X_PASSES):
             nc.sync.dma_start(out=w_words[:, 1 + g, :].bitcast(I32), in_=U_u_words[g].bitcast(I32))
-        gamma = const.tile([P, 2, H], BF16)
-        nc.sync.dma_start(
-            out=gamma[:].rearrange("p i n -> p (i n)"),
-            in_=ln_gamma.rearrange("i n -> (i n)").partition_broadcast(P),
-        )
+        load_first(slice(1, 2))
+        nc.sync.dma_start(out=rows[0:2, 0, :], in_=ln_beta)
+        nc.sync.dma_start(out=rows[0:1, 1:, :], in_=ln_gamma.rearrange("(o i) n -> o i n", o=1))
         load_first(slice(2, 4))
-        beta = const.tile([P, 2, H], BF16)
-        nc.sync.dma_start(
-            out=beta[:].rearrange("p i n -> p (i n)"),
-            in_=ln_beta.rearrange("i n -> (i n)").partition_broadcast(P),
-        )
-        beta_sum = const.tile([P, H], F32)
-        nc.gpsimd.tensor_tensor(out=beta_sum[:], in0=beta[:, 0, :], in1=beta[:, 1, :], op=ALU.add)
         nc.sync.dma_start(out=c_sb[0][:], in_=c_groups[0])
         load(1)
+        gamma = const.tile([P, 2, H], BF16)
+        beta_sum = const.tile([P, H], F32)
+
+        def spread_rows():
+            for plane, dst in ((1, gamma[:, 0, :]), (2, gamma[:, 1, :]), (0, beta_sum[:])):
+                bank = psum.tile([P, H], F32, name="diff_psum", bufs=2)
+                nc.tensor.matmul(bank[:], lhsT=ones[:], rhs=rows[:, plane, :], start=True, stop=True)
+                nc.vector.tensor_copy(out=dst, in_=bank[:])
 
         xT = {}
         x_grouped, h_grouped = {}, {}
@@ -311,7 +313,7 @@ def tile_layernormgrucell_pb_t_kernel(
             if 0 <= i < N_TILES:
                 stage(i)
 
-        early_diffs = {0: ((0, 2), (2, 1)), 1: ((3, 1), (4, 2)), 2: ((6, 2),), 3: ((8, 2),), 4: ((10, 2),), 5: ((12, 1),)}
+        early_diffs = {0: ((0, 2), (2, 1)), 1: ((3, 1), (4, 2)), 2: ((6, 2),), 3: ((8, 2),), 4: ((10, 2),), 5: ((12, 2),), 6: ((14, 1),)}
         for k in range(-3, N_TILES + 6):
             first_of_next_group = k + 3 + GROUP_TILES
             if first_of_next_group % GROUP_TILES == 0 and 2 * GROUP_TILES <= first_of_next_group < N_TILES:
@@ -319,6 +321,8 @@ def tile_layernormgrucell_pb_t_kernel(
             run(add_hidden_norm, k - 2)
             run(folded_matmuls, k + 1)
             run(matmuls, k + 1)
+            if k == -1:
+                spread_rows()
             run(sigmoid, k - 3)
             run(copy_x, k + 2)
             run(centre_h, k)

@@ -60,7 +60,7 @@ def tile_layernormgrucell_pb_t_kernel(
 
         w_scales = const.tile([P, 1 + X_PASSES, H], U8, align_bytes=64)
         nc.vector.memset(w_scales[:].rearrange("p w n -> p (w n)").bitcast(I32), 0)
-        neg_half = const.tile([P, 4], F32)
+        neg_half = const.tile([P, 2], F32)
         nc.vector.memset(neg_half[:], -0.5)
         ident = const.tile([P, P], F32)
         masks.make_identity(nc, ident[:])
@@ -104,19 +104,39 @@ def tile_layernormgrucell_pb_t_kernel(
         load(1)
         gamma = const.tile([P, 2, H], BF16)
         beta_sum = const.tile([P, H], F32)
+        columns = const.tile([P, 2, H // P], F32)
+
+        turn = psum.tile([P, H // P, P], F32, name="turn", bufs=1)
+
+        spread = {}
 
         def spread_rows():
-            for plane, dst in ((1, gamma[:, 0, :]), (2, gamma[:, 1, :]), (0, beta_sum[:])):
-                bank = psum.tile([P, H], F32, name="diff_psum", bufs=2)
-                nc.tensor.matmul(bank[:], lhsT=ones[:], rhs=rows[:, plane, :], start=True, stop=True)
-                nc.vector.tensor_copy(out=dst, in_=bank[:])
+            for plane, tag in ((0, "diff_psum"), (1, "acc_h"), (2, "acc_x")):
+                spread[plane] = psum.tile([P, H], F32, name="spread_%d" % plane, tag=tag, bufs=1 if plane == 0 else 2)
+                nc.tensor.matmul(spread[plane][:], lhsT=ones[:], rhs=rows[:, plane, :], start=True, stop=True)
+            for i, plane in enumerate((1, 0)):
+                for j in range(H // P):
+                    nc.tensor.matmul(
+                        turn[:, i, j : j + 1],
+                        lhsT=rows[:, plane, j * P : (j + 1) * P],
+                        rhs=ones[:, 0:1],
+                        start=True,
+                        stop=True,
+                    )
+
+        def keep_spread_rows():
+            nc.vector.tensor_copy(out=gamma[:, 0, :], in_=spread[1][:])
+            nc.vector.tensor_copy(out=gamma[:, 1, :], in_=spread[2][:])
+            nc.vector.tensor_copy(out=beta_sum[:], in_=spread[0][:])
+            nc.vector.tensor_copy(out=columns[:], in_=turn[:, 0:2, 0 : H // P])
 
         xT = {}
         x_grouped, h_grouped = {}, {}
         x_codes, x_scales, h_codes, h_scales = {}, {}, {}, {}
         acc_h, acc_x = {}, {}
-        neg_mean, sq_pair, sq_sum, rstd = {}, {}, {}, {}
+        neg_mean, sq_sum, rstd = {}, {}, {}
         hid, gate, diff = {}, {}, {}
+        shifts, normed, scaled = {}, {}, {}
         gate_pair, diff_pair = {}, {}
 
         shared_bank = psum.tile([P, 4, P], F32, name="shared_bank", bufs=1)
@@ -201,32 +221,42 @@ def tile_layernormgrucell_pb_t_kernel(
                         stop=(j == len(passes) - 1),
                     )
 
-        def means(i):
-            neg_mean[i] = small.tile([P, 2], F32, name="neg_mean")
-            for col in range(2):
-                scrap = unread.tile([P, P], F32, name="mean_scrap")
-                nc.scalar.activation(
-                    out=scrap[:],
-                    in_=folded[:, col, :],
-                    func=ACT.Identity,
-                    scale=-1.0 / H,
-                    accum_out=neg_mean[i][:, col : col + 1],
-                )
+        def mean(i, col):
+            if col == 0:
+                neg_mean[i] = small.tile([P, 2], F32, name="neg_mean")
+            scrap = unread.tile([P, P], F32, name="mean_scrap")
+            nc.scalar.activation(
+                out=scrap[:],
+                in_=folded[:, col, :],
+                func=ACT.Identity,
+                scale=-1.0 / H,
+                accum_out=neg_mean[i][:, col : col + 1],
+            )
 
-        def squares(i):
-            if i % 2 == 0:
-                sq_pair[i // 2] = small.tile([P, 2, 2], F32, name="sq_sum")
-            sq_sum[i] = sq_pair[i // 2][:, i % 2, :]
-            for col, acc in enumerate((acc_h[i], acc_x[i])):
-                scrap = unread.tile([P, H], F32, name="scrap")
-                nc.scalar.activation(
-                    out=scrap[:],
-                    in_=acc[:],
-                    func=ACT.Square,
-                    bias=neg_mean[i][:, col : col + 1],
-                    scale=1.0,
-                    accum_out=sq_sum[i][:, col : col + 1],
-                )
+        def square(i, col):
+            if col == 0:
+                sq_sum[i] = small.tile([P, 2], F32, name="sq_sum")
+            scrap = unread.tile([P, H], F32, name="scrap")
+            nc.scalar.activation(
+                out=scrap[:],
+                in_=(acc_h[i], acc_x[i])[col][:],
+                func=ACT.Square,
+                bias=neg_mean[i][:, col : col + 1],
+                scale=1.0,
+                accum_out=sq_sum[i][:, col : col + 1],
+            )
+
+        def mean_h(i):
+            mean(i, 0)
+
+        def mean_x(i):
+            mean(i, 1)
+
+        def square_h(i):
+            square(i, 0)
+
+        def square_x(i):
+            square(i, 1)
 
         def centre(i, col, acc, dst):
             nc.vector.scalar_tensor_tensor(
@@ -238,7 +268,48 @@ def tile_layernormgrucell_pb_t_kernel(
                 op1=ALU.mult,
             )
 
+        def turned(i):
+            return i % 3 == 0 and i > 0
+
+        def shift(i):
+            if turned(i):
+                shifts[i] = small.tile([P, 1], F32, name="shift")
+                nc.gpsimd.tensor_tensor(
+                    out=shifts[i][:], in0=neg_mean[i][:, 0:1], in1=rstd[i][:, 0:1], op=ALU.mult
+                )
+
+        def normalise(i):
+            if turned(i):
+                normed[i] = work.tile([P, H], F32, name="normed", bufs=2)
+                nc.scalar.activation(
+                    out=normed[i][:], in_=acc_h[i][:], func=ACT.Identity, scale=rstd[i][:, 0:1], bias=shifts[i][:]
+                )
+
+        def turn_over(i):
+            if turned(i):
+                for j in range(H // P):
+                    nc.tensor.transpose(turn[:, j, :], normed[i][:, j * P : (j + 1) * P], ident[:])
+
+        def scale_features(i):
+            if turned(i):
+                scaled[i] = work.tile([P, H // P, P], F32, name="scaled", bufs=2)
+                for j in range(H // P):
+                    nc.scalar.activation(
+                        out=scaled[i][:, j, :],
+                        in_=turn[:, j, :],
+                        func=ACT.Identity,
+                        scale=columns[:, 0, j : j + 1],
+                        bias=columns[:, 1, j : j + 1],
+                    )
+
+        def turn_back(i):
+            if turned(i):
+                for j in range(H // P):
+                    nc.tensor.transpose(turn[:, j, :], scaled[i][:, j, :], ident[:])
+
         def centre_h(i):
+            if turned(i):
+                return
             hid[i] = work.tile([P, H], F32, name="hid")
             centre(i, 0, acc_h[i], hid[i][:])
 
@@ -248,21 +319,13 @@ def tile_layernormgrucell_pb_t_kernel(
             gate[i] = gate_pair[i // 2][:, i % 2, :]
             centre(i, 1, acc_x[i], gate[i])
 
-        def inverse_deviations(i):
-            if i % 2 == 0:
-                return
-            var_eps = small.tile([P, 4], F32, name="var_eps")
+        def inverse_deviation(i):
+            var_eps = small.tile([P, 2], F32, name="var_eps")
             nc.gpsimd.tensor_scalar(
-                out=var_eps[:],
-                in0=sq_pair[i // 2][:].rearrange("p i n -> p (i n)"),
-                scalar1=1.0 / H,
-                scalar2=EPS,
-                op0=ALU.mult,
-                op1=ALU.add,
+                out=var_eps[:], in0=sq_sum[i][:], scalar1=1.0 / H, scalar2=EPS, op0=ALU.mult, op1=ALU.add
             )
-            rstd_pair = small.tile([P, 4], F32, name="rstd")
-            nc.gpsimd.tensor_tensor(out=rstd_pair[:], in0=var_eps[:], in1=neg_half[:], op=ALU.pow)
-            rstd[i - 1], rstd[i] = rstd_pair[:, 0:2], rstd_pair[:, 2:4]
+            rstd[i] = small.tile([P, 2], F32, name="rstd")
+            nc.gpsimd.tensor_tensor(out=rstd[i][:], in0=var_eps[:], in1=neg_half[:], op=ALU.pow)
 
         def vector_differences(first, count):
             g, t = divmod(first, GROUP_TILES)
@@ -280,19 +343,22 @@ def tile_layernormgrucell_pb_t_kernel(
             if i < VECTOR_DIFF_TILES:
                 return
             g, t = divmod(i, GROUP_TILES)
-            bank = psum.tile([P, H], F32, name="diff_psum", bufs=2)
+            bank = psum.tile([P, H], F32, name="diff_psum", bufs=1)
             diff[i] = bank[:]
             nc.tensor.matmul(diff[i], lhsT=ident_bf[:], rhs=c_sb[g][:, t, :], start=True, stop=False)
             nc.tensor.matmul(diff[i], lhsT=neg_ident_bf[:], rhs=h_sb[g][:, t, :], start=False, stop=True)
 
         def add_hidden_norm(i):
+            if turned(i):
+                return
             nc.vector.scalar_tensor_tensor(
                 out=hid[i][:], in0=hid[i][:], scalar=rstd[i][:, 0:1], in1=beta_sum[:], op0=ALU.mult, op1=ALU.add
             )
 
         def add_input_norm(i):
+            hidden_norm = turn[:].rearrange("p j n -> p (j n)") if turned(i) else hid[i][:]
             nc.vector.scalar_tensor_tensor(
-                out=gate[i], in0=gate[i], scalar=rstd[i][:, 1:2], in1=hid[i][:], op0=ALU.mult, op1=ALU.add
+                out=gate[i], in0=gate[i], scalar=rstd[i][:, 1:2], in1=hidden_norm, op0=ALU.mult, op1=ALU.add
             )
 
         def sigmoid(i):
@@ -313,31 +379,40 @@ def tile_layernormgrucell_pb_t_kernel(
             if 0 <= i < N_TILES:
                 stage(i)
 
-        early_diffs = {0: ((0, 2), (2, 1)), 1: ((3, 1), (4, 2)), 2: ((6, 2),), 3: ((8, 2),), 4: ((10, 2),), 5: ((12, 2),), 6: ((14, 1),)}
-        for k in range(-3, N_TILES + 6):
+        early_diffs = {0: (0, 2), 1: (2, 2), 2: (4, 2), 3: (6, 2), 8: (8, 2), 10: (10, 2), 12: (12, 2), 14: (14, 1)}
+        for k in range(-3, N_TILES + 5):
             first_of_next_group = k + 3 + GROUP_TILES
             if first_of_next_group % GROUP_TILES == 0 and 2 * GROUP_TILES <= first_of_next_group < N_TILES:
                 load(first_of_next_group // GROUP_TILES)
-            run(add_hidden_norm, k - 2)
+            run(transposes_h, k + 3)
+            run(inverse_deviation, k)
+            run(centre_x, k - 1)
+            run(turn_over, k - 1)
+            run(add_input_norm, k - 2)
             run(folded_matmuls, k + 1)
-            run(matmuls, k + 1)
-            if k == -1:
-                spread_rows()
-            run(sigmoid, k - 3)
             run(copy_x, k + 2)
-            run(centre_h, k)
-            run(add_state_and_store, k - 5)
-            run(centre_x, k)
+            run(matmuls, k + 1)
             run(quantise_h, k + 2)
             run(weigh_difference, k - 3)
-            run(quantise_x, k + 2)
-            for first, count in early_diffs.get(k, ()):
-                vector_differences(first, count)
-            run(add_input_norm, k - 2)
-            run(inverse_deviations, k)
-            run(means, k + 1)
-            run(transposes_h, k + 3)
-            run(transposes_x, k + 3)
-            run(tensor_difference, k - 2)
-            run(squares, k + 1)
+            if k in early_diffs:
+                vector_differences(*early_diffs[k])
+            run(scale_features, k - 1)
+            run(add_hidden_norm, k - 1)
+            run(sigmoid, k - 2)
+            run(mean_h, k + 1)
+            run(add_state_and_store, k - 5)
             run(copy_h, k + 3)
+            run(mean_x, k + 1)
+            run(square_h, k + 1)
+            run(shift, k)
+            run(normalise, k)
+            run(turn_back, k - 1)
+            run(centre_h, k)
+            run(square_x, k + 1)
+            run(quantise_x, k + 2)
+            if k == -1:
+                keep_spread_rows()
+            run(tensor_difference, k - 2)
+            run(transposes_x, k + 3)
+            if k == -2:
+                spread_rows()

@@ -139,8 +139,8 @@ def tile_layernormgrucell_pb_t_kernel(
         shifts, normed, scaled = {}, {}, {}
         gate_pair, diff_pair = {}, {}
 
-        shared_bank = psum.tile([P, 4, P], F32, name="shared_bank", bufs=1)
-        h_words_bank, folded = shared_bank[:, 0:2, :], shared_bank[:, 2:4, :]
+        shared_bank = psum.tile([P, 3, P], F32, name="shared_bank", bufs=1)
+        h_words_bank, folded = shared_bank[:, 0:2, :], shared_bank[:, 2, :]
 
         def transposes_h(i):
             g, t = divmod(i, GROUP_TILES)
@@ -182,7 +182,7 @@ def tile_layernormgrucell_pb_t_kernel(
             x_scales[i] = quant.tile([P, X_PASSES * P], U8, name="x_scales", align_bytes=64)
             nc.vector.quantize_mx(out=x_codes[i][:].bitcast(FP8X4), scales=x_scales[i][:], in_=x_grouped[i][:])
 
-        def matmuls(i):
+        def matmul_h(i):
             acc_h[i] = psum.tile([P, H], F32, name="acc_h")
             nc.tensor.matmul_mx(
                 out=acc_h[i][:],
@@ -193,6 +193,8 @@ def tile_layernormgrucell_pb_t_kernel(
                 start=True,
                 stop=True,
             )
+
+        def matmul_x(i):
             acc_x[i] = psum.tile([P, H], F32, name="acc_x")
             for s in range(X_PASSES):
                 cols = slice(s * P, (s + 1) * P)
@@ -207,27 +209,25 @@ def tile_layernormgrucell_pb_t_kernel(
                 )
 
         def folded_matmuls(i):
-            for col, codes, scales, weights in ((0, h_codes[i], h_scales[i], (0,)), (1, x_codes[i], x_scales[i], (1, 2))):
-                passes = [(s, w, q) for s, w in enumerate(weights) for q in range(H // P)]
-                for j, (s, w, q) in enumerate(passes):
-                    rows = slice(s * P, (s + 1) * P)
-                    nc.tensor.matmul_mx(
-                        out=folded[:, col, :],
-                        lhsT=codes[:, rows].bitcast(FP8X4),
-                        lhsT_scale=scales[:, rows],
-                        rhs=w_words[:, w, 2 * q * P : 2 * (q + 1) * P].bitcast(FP4X4),
-                        rhs_scale=w_scales[:, w, q * P : (q + 1) * P],
-                        start=(j == 0),
-                        stop=(j == len(passes) - 1),
-                    )
+            for q in range(H // P):
+                nc.tensor.matmul_mx(
+                    out=folded,
+                    lhsT=h_codes[i][:].bitcast(FP8X4),
+                    lhsT_scale=h_scales[i][:],
+                    rhs=w_words[:, 0, 2 * q * P : 2 * (q + 1) * P].bitcast(FP4X4),
+                    rhs_scale=w_scales[:, 0, q * P : (q + 1) * P],
+                    start=(q == 0),
+                    stop=(q == H // P - 1),
+                )
 
         def mean(i, col):
             if col == 0:
                 neg_mean[i] = small.tile([P, 2], F32, name="neg_mean")
-            scrap = unread.tile([P, P], F32, name="mean_scrap")
+            source = folded if col == 0 else acc_x[i][:]
+            scrap = unread.tile([P, (P, H)[col]], F32, name="mean_scrap")
             nc.scalar.activation(
                 out=scrap[:],
-                in_=folded[:, col, :],
+                in_=source,
                 func=ACT.Identity,
                 scale=-1.0 / H,
                 accum_out=neg_mean[i][:, col : col + 1],
@@ -269,7 +269,7 @@ def tile_layernormgrucell_pb_t_kernel(
             )
 
         def turned(i):
-            return i % 3 == 0 and i > 0
+            return i % 5 == 3
 
         def shift(i):
             if turned(i):
@@ -385,34 +385,35 @@ def tile_layernormgrucell_pb_t_kernel(
             if first_of_next_group % GROUP_TILES == 0 and 2 * GROUP_TILES <= first_of_next_group < N_TILES:
                 load(first_of_next_group // GROUP_TILES)
             run(transposes_h, k + 3)
-            run(inverse_deviation, k)
-            run(centre_x, k - 1)
-            run(turn_over, k - 1)
-            run(add_input_norm, k - 2)
-            run(folded_matmuls, k + 1)
             run(copy_x, k + 2)
-            run(matmuls, k + 1)
-            run(quantise_h, k + 2)
+            run(centre_x, k - 1)
+            run(folded_matmuls, k + 1)
+            run(add_input_norm, k - 2)
+            run(copy_h, k + 3)
+            run(matmul_x, k + 1)
+            run(mean_h, k + 1)
+            run(turn_over, k - 1)
             run(weigh_difference, k - 3)
+            run(scale_features, k - 1)
+            run(sigmoid, k - 2)
+            run(mean_x, k + 1)
+            run(matmul_h, k + 1)
+            run(square_h, k + 1)
+            run(quantise_h, k + 2)
             if k in early_diffs:
                 vector_differences(*early_diffs[k])
-            run(scale_features, k - 1)
-            run(add_hidden_norm, k - 1)
-            run(sigmoid, k - 2)
-            run(mean_h, k + 1)
-            run(add_state_and_store, k - 5)
-            run(copy_h, k + 3)
-            run(mean_x, k + 1)
-            run(square_h, k + 1)
-            run(shift, k)
-            run(normalise, k)
-            run(turn_back, k - 1)
-            run(centre_h, k)
-            run(square_x, k + 1)
-            run(quantise_x, k + 2)
-            if k == -1:
-                keep_spread_rows()
             run(tensor_difference, k - 2)
+            run(add_state_and_store, k - 5)
+            run(add_hidden_norm, k - 1)
+            run(centre_h, k)
+            run(inverse_deviation, k)
             run(transposes_x, k + 3)
             if k == -2:
                 spread_rows()
+            run(quantise_x, k + 2)
+            if k == -1:
+                keep_spread_rows()
+            run(shift, k)
+            run(normalise, k)
+            run(turn_back, k - 1)
+            run(square_x, k + 1)

@@ -269,7 +269,7 @@ def tile_layernormgrucell_pb_t_kernel(
             )
 
         def turned(i):
-            return i % 5 == 3
+            return i % 10 == 8
 
         def shift(i):
             if turned(i):
@@ -368,12 +368,17 @@ def tile_layernormgrucell_pb_t_kernel(
             nc.vector.tensor_tensor(out=gate[i], in0=gate[i], in1=diff[i], op=ALU.mult)
 
         def add_state_and_store(i):
-            if i % 2 == 1:
+            if i >= N_TILES - 2:
+                count = 1
+            elif i % 2 == 0:
+                count = 2
+            else:
                 return
             g, t = divmod(i, GROUP_TILES)
-            pair = gate_pair[i // 2]
-            nc.vector.tensor_tensor(out=pair[:], in0=pair[:], in1=h_sb[g][:, t : t + 2, :], op=ALU.add)
-            nc.sync.dma_start(out=out_groups[g][:, t : t + 2, :], in_=pair[:])
+            rows_out = gate_pair[i // 2][:, i % 2 : i % 2 + count, :]
+            tiles = slice(t, t + count)
+            nc.vector.tensor_tensor(out=rows_out, in0=rows_out, in1=h_sb[g][:, tiles, :], op=ALU.add)
+            nc.sync.dma_start(out=out_groups[g][:, tiles, :], in_=rows_out)
 
         def run(stage, i):
             if 0 <= i < N_TILES:

from contextlib import ExitStack

import concourse.masks as masks
import concourse.mybir as mybir

F32 = mybir.dt.float32
BF16 = mybir.dt.bfloat16
I32 = mybir.dt.int32
U32 = mybir.dt.uint32
U8 = mybir.dt.uint8
FP8X4 = mybir.dt.float8_e4m3fn_x4
FP4X4 = mybir.dt.float4_e2m1fn_x4
ACT = mybir.ActivationFunctionType
ALU = mybir.AluOpType

P = 128
ROWS, IN, H = 4096, 1024, 512
EPS = 1e-5
K_PASS = 4 * P
X_PASSES = IN // K_PASS
WORDS = K_PASS // 2
GROUP_TILES = 4
N_GROUPS = ROWS // (P * GROUP_TILES)
N_TILES = ROWS // P
VECTOR_DIFF_TILES = 15

FLOPS = 2 * ROWS * H * (H + IN)


def tile_layernormgrucell_pb_t_kernel(
    tc, x, h, c, W_u_words, W_u_scales, U_u_words, U_u_scales, ln_gamma, ln_beta, out
):
    nc = tc.nc

    x_groups = x.rearrange("(g p t) k -> g p t k", p=P, t=GROUP_TILES)
    h_groups = h.rearrange("(g p t) k -> g p t k", p=P, t=GROUP_TILES)
    c_groups = c.rearrange("(g p t) k -> g p t k", p=P, t=GROUP_TILES)
    out_groups = out.rearrange("(g p t) n -> g p t n", p=P, t=GROUP_TILES)

    with ExitStack() as ctx:
        const = ctx.enter_context(tc.tile_pool(name="const", bufs=1))
        x_pool = ctx.enter_context(tc.tile_pool(name="x_pool", bufs=3))
        hc_pool = ctx.enter_context(tc.tile_pool(name="hc_pool", bufs=4))
        quant = ctx.enter_context(tc.tile_pool(name="quant", bufs=3))
        unread = ctx.enter_context(tc.tile_pool(name="unread", bufs=4))
        small = ctx.enter_context(tc.tile_pool(name="small", bufs=4))
        work = ctx.enter_context(tc.tile_pool(name="work", bufs=8))
        psum = ctx.enter_context(tc.psum_pool(name="psum", bufs=2))
        ctx.enter_context(tc.manual_schedule())

        x_sb, h_sb, c_sb = {}, {}, {}

        def load(g):
            h_sb[g] = hc_pool.tile([P, GROUP_TILES, H], BF16, name="h_rows")
            nc.sync.dma_start(out=h_sb[g][:], in_=h_groups[g])
            x_sb[g] = x_pool.tile([P, GROUP_TILES, IN], BF16, name="x_rows")
            nc.sync.dma_start(out=x_sb[g][:], in_=x_groups[g])
            c_sb[g] = hc_pool.tile([P, GROUP_TILES, H], BF16, name="c_rows")
            nc.sync.dma_start(out=c_sb[g][:], in_=c_groups[g])

        w_scales = const.tile([P, 1 + X_PASSES, H], U8, align_bytes=64)
        nc.vector.memset(w_scales[:].rearrange("p w n -> p (w n)").bitcast(I32), 0)
        neg_half = const.tile([P, 2], F32)
        nc.vector.memset(neg_half[:], -0.5)
        ident = const.tile([P, P], F32)
        masks.make_identity(nc, ident[:])
        rows = const.tile([P, 3, H], BF16)
        nc.gpsimd.memset(rows[:], 0.0)
        ones = const.tile([P, P], BF16)
        nc.gpsimd.memset(ones[:], 1.0)
        ident_bf = const.tile([P, P], BF16)
        nc.vector.tensor_copy(out=ident_bf[:], in_=ident[:])
        neg_ident_bf = const.tile([P, P], BF16)
        nc.vector.tensor_scalar(out=neg_ident_bf[:], in0=ident[:], scalar1=-1.0, scalar2=None, op0=ALU.mult)

        x_sb[0] = x_pool.tile([P, GROUP_TILES, IN], BF16, name="x_rows")
        h_sb[0] = hc_pool.tile([P, GROUP_TILES, H], BF16, name="h_rows")
        c_sb[0] = hc_pool.tile([P, GROUP_TILES, H], BF16, name="c_rows")

        def load_first(tiles):
            nc.sync.dma_start(out=h_sb[0][:, tiles, :], in_=h_groups[0][:, tiles, :])
            nc.sync.dma_start(out=x_sb[0][:, tiles, :], in_=x_groups[0][:, tiles, :])

        load_first(slice(0, 1))
        w_words = const.tile([P, 1 + X_PASSES, 2 * H], U8, align_bytes=64)
        for q in range(4):
            nc.sync.dma_start(
                out=w_scales[32 * q : 32 * q + 4, 0, :].bitcast(I32),
                in_=W_u_scales[0, 4 * q : 4 * q + 4, :].bitcast(I32),
            )
        for q in range(4):
            nc.sync.dma_start(
                out=w_scales[32 * q : 32 * q + 4, 1:, :].bitcast(I32),
                in_=U_u_scales[:, 4 * q : 4 * q + 4, :].rearrange("g r n -> r g n").bitcast(I32),
            )
        nc.sync.dma_start(out=w_words[:, 0, :].bitcast(I32), in_=W_u_words[0].bitcast(I32))
        for g in range(X_PASSES):
            nc.sync.dma_start(out=w_words[:, 1 + g, :].bitcast(I32), in_=U_u_words[g].bitcast(I32))
        load_first(slice(1, 2))
        nc.sync.dma_start(out=rows[0:2, 0, :], in_=ln_beta)
        nc.sync.dma_start(out=rows[0:1, 1:, :], in_=ln_gamma.rearrange("(o i) n -> o i n", o=1))
        load_first(slice(2, 4))
        nc.sync.dma_start(out=c_sb[0][:], in_=c_groups[0])
        load(1)
        gamma = const.tile([P, 2, H], BF16)
        beta_sum = const.tile([P, H], F32)
        columns = const.tile([P, 2, H // P], F32)

        turn = psum.tile([P, H // P, P], F32, name="turn", bufs=1)

        spread = {}

        def spread_rows():
            for plane, tag in ((0, "diff_psum"), (1, "acc_h"), (2, "acc_x")):
                spread[plane] = psum.tile([P, H], F32, name="spread_%d" % plane, tag=tag, bufs=1 if plane == 0 else 2)
                nc.tensor.matmul(spread[plane][:], lhsT=ones[:], rhs=rows[:, plane, :], start=True, stop=True)
            for i, plane in enumerate((1, 0)):
                for j in range(H // P):
                    nc.tensor.matmul(
                        turn[:, i, j : j + 1],
                        lhsT=rows[:, plane, j * P : (j + 1) * P],
                        rhs=ones[:, 0:1],
                        start=True,
                        stop=True,
                    )

        def keep_spread_rows():
            nc.vector.tensor_copy(out=gamma[:, 0, :], in_=spread[1][:])
            nc.vector.tensor_copy(out=gamma[:, 1, :], in_=spread[2][:])
            nc.vector.tensor_copy(out=beta_sum[:], in_=spread[0][:])
            nc.vector.tensor_copy(out=columns[:], in_=turn[:, 0:2, 0 : H // P])

        xT = {}
        x_grouped, h_grouped = {}, {}
        x_codes, x_scales, h_codes, h_scales = {}, {}, {}, {}
        acc_h, acc_x = {}, {}
        neg_mean, sq_sum, rstd = {}, {}, {}
        hid, gate, diff = {}, {}, {}
        shifts, normed, scaled = {}, {}, {}
        gate_pair, diff_pair = {}, {}

        shared_bank = psum.tile([P, 3, P], F32, name="shared_bank", bufs=1)
        h_words_bank, folded = shared_bank[:, 0:2, :], shared_bank[:, 2, :]

        def transposes_h(i):
            g, t = divmod(i, GROUP_TILES)
            h_words = h_sb[g][:, t, :].bitcast(F32)
            for u in range(2):
                nc.tensor.transpose(h_words_bank[:, u, :], h_words[:, u:WORDS:2], ident[:])

        def transposes_x(i):
            g, t = divmod(i, GROUP_TILES)
            x_words = x_sb[g][:, t, :].bitcast(F32)
            xT[i] = psum.tile([P, X_PASSES, 2, P], F32, name="xT", bufs=1)
            for s in range(X_PASSES):
                for u in range(2):
                    nc.tensor.transpose(
                        xT[i][:, s, u, :], x_words[:, s * WORDS + u : (s + 1) * WORDS : 2], ident[:]
                    )

        def copy_h(i):
            h_grouped[i] = quant.tile([P, 4 * P], BF16, name="h_grouped", align_bytes=64)
            nc.scalar.copy(
                out=h_grouped[i][:].bitcast(F32).rearrange("p (r u) -> p r u", u=2),
                in_=h_words_bank.rearrange("p u r -> p r u"),
            )

        def copy_x(i):
            x_grouped[i] = quant.tile([P, X_PASSES * 4 * P], BF16, name="x_grouped", align_bytes=64)
            nc.scalar.copy(
                out=x_grouped[i][:].bitcast(F32).rearrange("p (s r u) -> p s r u", s=X_PASSES, u=2),
                in_=xT[i][:].rearrange("p s u r -> p s r u"),
            )

        def quantise_h(i):
            h_codes[i] = quant.tile([P, P], U32, name="h_codes", align_bytes=64)
            h_scales[i] = quant.tile([P, P], U8, name="h_scales", align_bytes=64)
            nc.vector.quantize_mx(out=h_codes[i][:].bitcast(FP8X4), scales=h_scales[i][:], in_=h_grouped[i][:])

        def quantise_x(i):
            x_codes[i] = quant.tile([P, X_PASSES * P], U32, name="x_codes", align_bytes=64)
            x_scales[i] = quant.tile([P, X_PASSES * P], U8, name="x_scales", align_bytes=64)
            nc.vector.quantize_mx(out=x_codes[i][:].bitcast(FP8X4), scales=x_scales[i][:], in_=x_grouped[i][:])

        def matmul_h(i):
            acc_h[i] = psum.tile([P, H], F32, name="acc_h")
            nc.tensor.matmul_mx(
                out=acc_h[i][:],
                lhsT=h_codes[i][:].bitcast(FP8X4),
                lhsT_scale=h_scales[i][:],
                rhs=w_words[:, 0, :].bitcast(FP4X4),
                rhs_scale=w_scales[:, 0, :],
                start=True,
                stop=True,
            )

        def matmul_x(i):
            acc_x[i] = psum.tile([P, H], F32, name="acc_x")
            for s in range(X_PASSES):
                cols = slice(s * P, (s + 1) * P)
                nc.tensor.matmul_mx(
                    out=acc_x[i][:],
                    lhsT=x_codes[i][:, cols].bitcast(FP8X4),
                    lhsT_scale=x_scales[i][:, cols],
                    rhs=w_words[:, 1 + s, :].bitcast(FP4X4),
                    rhs_scale=w_scales[:, 1 + s, :],
                    start=(s == 0),
                    stop=(s == X_PASSES - 1),
                )

        def folded_matmuls(i):
            for q in range(H // P):
                nc.tensor.matmul_mx(
                    out=folded,
                    lhsT=h_codes[i][:].bitcast(FP8X4),
                    lhsT_scale=h_scales[i][:],
                    rhs=w_words[:, 0, 2 * q * P : 2 * (q + 1) * P].bitcast(FP4X4),
                    rhs_scale=w_scales[:, 0, q * P : (q + 1) * P],
                    start=(q == 0),
                    stop=(q == H // P - 1),
                )

        def mean(i, col):
            if col == 0:
                neg_mean[i] = small.tile([P, 2], F32, name="neg_mean")
            source = folded if col == 0 else acc_x[i][:]
            scrap = unread.tile([P, (P, H)[col]], F32, name="mean_scrap")
            nc.scalar.activation(
                out=scrap[:],
                in_=source,
                func=ACT.Identity,
                scale=-1.0 / H,
                accum_out=neg_mean[i][:, col : col + 1],
            )

        def square(i, col):
            if col == 0:
                sq_sum[i] = small.tile([P, 2], F32, name="sq_sum")
            scrap = unread.tile([P, H], F32, name="scrap")
            nc.scalar.activation(
                out=scrap[:],
                in_=(acc_h[i], acc_x[i])[col][:],
                func=ACT.Square,
                bias=neg_mean[i][:, col : col + 1],
                scale=1.0,
                accum_out=sq_sum[i][:, col : col + 1],
            )

        def mean_h(i):
            mean(i, 0)

        def mean_x(i):
            mean(i, 1)

        def square_h(i):
            square(i, 0)

        def square_x(i):
            square(i, 1)

        def centre(i, col, acc, dst):
            nc.vector.scalar_tensor_tensor(
                out=dst,
                in0=acc[:],
                scalar=neg_mean[i][:, col : col + 1],
                in1=gamma[:, col, :],
                op0=ALU.add,
                op1=ALU.mult,
            )

        def turned(i):
            return i % 10 == 8

        def shift(i):
            if turned(i):
                shifts[i] = small.tile([P, 1], F32, name="shift")
                nc.gpsimd.tensor_tensor(
                    out=shifts[i][:], in0=neg_mean[i][:, 0:1], in1=rstd[i][:, 0:1], op=ALU.mult
                )

        def normalise(i):
            if turned(i):
                normed[i] = work.tile([P, H], F32, name="normed", bufs=2)
                nc.scalar.activation(
                    out=normed[i][:], in_=acc_h[i][:], func=ACT.Identity, scale=rstd[i][:, 0:1], bias=shifts[i][:]
                )

        def turn_over(i):
            if turned(i):
                for j in range(H // P):
                    nc.tensor.transpose(turn[:, j, :], normed[i][:, j * P : (j + 1) * P], ident[:])

        def scale_features(i):
            if turned(i):
                scaled[i] = work.tile([P, H // P, P], F32, name="scaled", bufs=2)
                for j in range(H // P):
                    nc.scalar.activation(
                        out=scaled[i][:, j, :],
                        in_=turn[:, j, :],
                        func=ACT.Identity,
                        scale=columns[:, 0, j : j + 1],
                        bias=columns[:, 1, j : j + 1],
                    )

        def turn_back(i):
            if turned(i):
                for j in range(H // P):
                    nc.tensor.transpose(turn[:, j, :], scaled[i][:, j, :], ident[:])

        def centre_h(i):
            if turned(i):
                return
            hid[i] = work.tile([P, H], F32, name="hid")
            centre(i, 0, acc_h[i], hid[i][:])

        def centre_x(i):
            if i % 2 == 0:
                gate_pair[i // 2] = work.tile([P, 2, H], F32, name="gate", bufs=6)
            gate[i] = gate_pair[i // 2][:, i % 2, :]
            centre(i, 1, acc_x[i], gate[i])

        def inverse_deviation(i):
            var_eps = small.tile([P, 2], F32, name="var_eps")
            nc.gpsimd.tensor_scalar(
                out=var_eps[:], in0=sq_sum[i][:], scalar1=1.0 / H, scalar2=EPS, op0=ALU.mult, op1=ALU.add
            )
            rstd[i] = small.tile([P, 2], F32, name="rstd")
            nc.gpsimd.tensor_tensor(out=rstd[i][:], in0=var_eps[:], in1=neg_half[:], op=ALU.pow)

        def vector_differences(first, count):
            g, t = divmod(first, GROUP_TILES)
            wide = work.tile([P, count, H], F32, name="diff_%d" % first, bufs=1)
            nc.vector.tensor_tensor(
                out=wide[:],
                in0=c_sb[g][:, t : t + count, :],
                in1=h_sb[g][:, t : t + count, :],
                op=ALU.subtract,
            )
            for j in range(count):
                diff[first + j] = wide[:, j, :]

        def tensor_difference(i):
            if i < VECTOR_DIFF_TILES:
                return
            g, t = divmod(i, GROUP_TILES)
            bank = psum.tile([P, H], F32, name="diff_psum", bufs=1)
            diff[i] = bank[:]
            nc.tensor.matmul(diff[i], lhsT=ident_bf[:], rhs=c_sb[g][:, t, :], start=True, stop=False)
            nc.tensor.matmul(diff[i], lhsT=neg_ident_bf[:], rhs=h_sb[g][:, t, :], start=False, stop=True)

        def add_hidden_norm(i):
            if turned(i):
                return
            nc.vector.scalar_tensor_tensor(
                out=hid[i][:], in0=hid[i][:], scalar=rstd[i][:, 0:1], in1=beta_sum[:], op0=ALU.mult, op1=ALU.add
            )

        def add_input_norm(i):
            hidden_norm = turn[:].rearrange("p j n -> p (j n)") if turned(i) else hid[i][:]
            nc.vector.scalar_tensor_tensor(
                out=gate[i], in0=gate[i], scalar=rstd[i][:, 1:2], in1=hidden_norm, op0=ALU.mult, op1=ALU.add
            )

        def sigmoid(i):
            nc.scalar.activation(out=gate[i], in_=gate[i], func=ACT.Sigmoid)

        def weigh_difference(i):
            nc.vector.tensor_tensor(out=gate[i], in0=gate[i], in1=diff[i], op=ALU.mult)

        def add_state_and_store(i):
            if i >= N_TILES - 2:
                count = 1
            elif i % 2 == 0:
                count = 2
            else:
                return
            g, t = divmod(i, GROUP_TILES)
            rows_out = gate_pair[i // 2][:, i % 2 : i % 2 + count, :]
            tiles = slice(t, t + count)
            nc.vector.tensor_tensor(out=rows_out, in0=rows_out, in1=h_sb[g][:, tiles, :], op=ALU.add)
            nc.sync.dma_start(out=out_groups[g][:, tiles, :], in_=rows_out)

        def run(stage, i):
            if 0 <= i < N_TILES:
                stage(i)

        early_diffs = {0: (0, 2), 1: (2, 2), 2: (4, 2), 3: (6, 2), 8: (8, 2), 10: (10, 2), 12: (12, 2), 14: (14, 1)}
        for k in range(-3, N_TILES + 5):
            first_of_next_group = k + 3 + GROUP_TILES
            if first_of_next_group % GROUP_TILES == 0 and 2 * GROUP_TILES <= first_of_next_group < N_TILES:
                load(first_of_next_group // GROUP_TILES)
            run(transposes_h, k + 3)
            run(copy_x, k + 2)
            run(centre_x, k - 1)
            run(folded_matmuls, k + 1)
            run(add_input_norm, k - 2)
            run(copy_h, k + 3)
            run(matmul_x, k + 1)
            run(mean_h, k + 1)
            run(turn_over, k - 1)
            run(weigh_difference, k - 3)
            run(scale_features, k - 1)
            run(sigmoid, k - 2)
            run(mean_x, k + 1)
            run(matmul_h, k + 1)
            run(square_h, k + 1)
            run(quantise_h, k + 2)
            if k in early_diffs:
                vector_differences(*early_diffs[k])
            run(tensor_difference, k - 2)
            run(add_state_and_store, k - 5)
            run(add_hidden_norm, k - 1)
            run(centre_h, k)
            run(inverse_deviation, k)
            run(transposes_x, k + 3)
            if k == -2:
                spread_rows()
            run(quantise_x, k + 2)
            if k == -1:
                keep_spread_rows()
            run(shift, k)
            run(normalise, k)
            run(turn_back, k - 1)
            run(square_x, k + 1)
